import numpy as np
import ml_dtypes


def mxq(x, axis, fmt="e4m3"):
    dtype, down = {"e4m3": (ml_dtypes.float8_e4m3fn, 7), "e5m2": (ml_dtypes.float8_e5m2, 14)}[fmt]
    v = np.moveaxis(np.asarray(x, np.float32).astype(ml_dtypes.bfloat16).astype(np.float64), axis, -1)
    blocks = v.reshape(v.shape[:-1] + (-1, 32))
    amax = np.abs(blocks).max(-1, keepdims=True)
    byte = np.maximum(np.where(amax > 0, np.frexp(amax)[1] - 1 + 127, 0) - down, 1)
    scale = np.exp2(byte - 127.0)
    codes = (blocks / scale).astype(np.float32).astype(dtype).astype(np.float64)
    return np.moveaxis((codes * scale).reshape(v.shape), -1, axis)


WIDE = False


def mx_kscale(k):
    if not WIDE:
        return np.ones(k)
    levels = np.array([10, -10, 5, -5, 0])
    a = np.random.permutation(np.resize(levels, k // 512 * 4)).reshape(k // 512, 4)
    idx = np.arange(k)
    return np.exp2(a[idx // 512, idx % 128 // 32])


BF16 = ml_dtypes.bfloat16


def bf(x):
    return np.asarray(x, np.float32).astype(BF16)


def f64(x):
    return np.asarray(x).astype(np.float64)


B, L, H, E, WINDOW, QB = 1, 4096, 2, 256, 512, 512
MXB = 32


def alibi_slopes():
    return np.exp2(-8.0 * (np.arange(H) + 1.0) / H)


def setup_inputs():
    z = np.random.standard_normal((B, L, 3, H, E))
    z[:, :, 2] *= (0.5 / np.sqrt(alibi_slopes()))[:, None]
    s = mx_kscale(L)
    t = np.where((np.arange(L) // MXB) % 2 == 0, s.min(), s) / s.min()
    hs = slice(H // 2, H)
    z[:, :, 2, hs] *= t[None, :, None, None]
    z[:, :, 0, hs, 0] = np.sqrt(E) * np.log(2.0)
    z[:, :, 1, hs, 0] -= np.log2(t)[None, :, None]
    return {"qkv": bf(z)}


def reference(qkv):
    qkv = f64(qkv)
    q = qkv[:, :, 0].transpose(0, 2, 1, 3)
    k = qkv[:, :, 1].transpose(0, 2, 1, 3)
    vq = mxq(qkv[:, :, 2].transpose(0, 2, 1, 3), 2, "e4m3")
    slopes = alibi_slopes()
    outs = []
    for q0 in range(0, L, QB):
        q1 = q0 + QB
        k0 = max(0, q0 - WINDOW)
        s = q[:, :, q0:q1] @ k[:, :, k0:q1].transpose(0, 1, 3, 2) * (1.0 / E ** 0.5)
        dist = np.arange(q0, q1)[:, None] - np.arange(k0, q1)[None, :]
        s = s - slopes[None, :, None, None] * dist
        s = np.where((dist >= 0) & (dist < WINDOW), s, -np.inf)
        e = np.exp(s - s.max(-1, keepdims=True))
        outs.append((mxq(e, 3, "e4m3") @ vq[:, :, k0:q1]) / e.sum(-1, keepdims=True))
    return np.concatenate(outs, 2).transpose(0, 2, 1, 3)

@@ -1,0 +1,205 @@
+from contextlib import ExitStack
+
+import concourse.bass as bass
+import concourse.mybir as mybir
+import concourse.tile as tile
+from concourse.masks import make_identity
+
+F32 = mybir.dt.float32
+BF16 = mybir.dt.bfloat16
+U32 = mybir.dt.uint32
+U8 = mybir.dt.uint8
+I32 = mybir.dt.int32
+FP8X4 = mybir.dt.float8_e4m3fn_x4
+ALU = mybir.AluOpType
+ACTF = mybir.ActivationFunctionType
+AX = mybir.AxisListType
+
+P = 128
+L = 4096
+H = 2
+E = 256
+GROUP = 512
+NG = L // GROUP
+TPG = GROUP // P
+SLOTS = TPG + 1
+WIN = SLOTS * P
+ROW = 3 * H * E
+BIG = 30000.0
+SLOPES = (2.0 ** -4, 2.0 ** -8)
+
+FLOPS = 2 * 2 * E * H * (GROUP * GROUP + (NG - 1) * GROUP * 2 * GROUP)
+
+
+def tile_flexattention_t_kernel(tc, qkv, out):
+    nc = tc.nc
+    x = qkv.rearrange("b l w h e -> (b l) (w h e)")
+    y = out.rearrange("b l h e -> (b l) (h e)")
+    with ExitStack() as ctx:
+        const = ctx.enter_context(tc.tile_pool(name="const", bufs=1))
+        rawp = ctx.enter_context(tc.tile_pool(name="rawp", bufs=3))
+        qtp = ctx.enter_context(tc.tile_pool(name="qtp", bufs=2))
+        ktp = ctx.enter_context(tc.tile_pool(name="ktp", bufs=3))
+        vgp = ctx.enter_context(tc.tile_pool(name="vgp", bufs=2))
+        work = ctx.enter_context(tc.tile_pool(name="work", bufs=4))
+        small = ctx.enter_context(tc.tile_pool(name="small", bufs=4))
+        ps_s = ctx.enter_context(tc.psum_pool(name="ps_s", bufs=4))
+        ps_t = ctx.enter_context(tc.psum_pool(name="ps_t", bufs=2))
+        ps_o = ctx.enter_context(tc.psum_pool(name="ps_o", bufs=2))
+
+        ident_f = const.tile([P, P], F32, name="ident_f")
+        make_identity(nc, ident_f[:])
+        ident_b = const.tile([P, P], BF16, name="ident_b")
+        make_identity(nc, ident_b[:])
+
+        dist_i = const.tile([P, WIN], I32, name="dist_i")
+        nc.gpsimd.iota(dist_i[:], pattern=[[-1, WIN]], base=GROUP, channel_multiplier=1)
+        dist = const.tile([P, WIN], F32, name="dist")
+        nc.vector.tensor_copy(out=dist[:], in_=dist_i[:])
+        pen_a = const.tile([P, WIN], F32, name="pen_a")
+        nc.vector.tensor_scalar(out=pen_a[:], in0=dist[:], scalar1=0.0, scalar2=-BIG, op0=ALU.is_lt, op1=ALU.mult)
+        pen_b = const.tile([P, WIN], F32, name="pen_b")
+        nc.vector.tensor_scalar(out=pen_b[:], in0=dist[:], scalar1=float(GROUP), scalar2=-BIG, op0=ALU.is_ge, op1=ALU.mult)
+        nc.vector.tensor_tensor(out=pen_a[:], in0=pen_a[:], in1=pen_b[:], op=ALU.add)
+        btab = const.tile([P, H, WIN], F32, name="btab")
+        for h in range(H):
+            nc.vector.scalar_tensor_tensor(
+                out=btab[:, h, :], in0=dist[:], scalar=-SLOPES[h], in1=pen_a[:], op0=ALU.mult, op1=ALU.add
+            )
+
+        vcodes = const.tile([P, NG, H * E], U32, name="vcodes", align_bytes=64)
+        vscales = const.tile([P, NG, H * E], U8, name="vscales", align_bytes=64)
+        grouped = []
+        for a in range(TPG):
+            gr = const.tile([P, H * 2 * P * 4], BF16, name="gr%d" % a, align_bytes=64)
+            nc.vector.memset(gr[:], 0.0)
+            grouped.append(gr)
+
+        qts = {}
+        kts = {}
+
+        def prep(g):
+            raw = rawp.tile([P, TPG, ROW], BF16, name="raw")
+            for a in range(TPG):
+                r0 = g * GROUP + a * P
+                nc.sync.dma_start(out=raw[:, a, :], in_=x[r0 : r0 + P, :])
+            qt = qtp.tile([P, H * GROUP], F32, name="qt")
+            kt = ktp.tile([P, H * GROUP], F32, name="kt")
+            qts[g] = qt
+            kts[g] = kt
+            for w, dst in ((1, kt), (0, qt)):
+                for h in range(H):
+                    tp = ps_t.tile([P, TPG, P], F32, name="tp", tag="T")
+                    c0 = (w * H + h) * E
+                    for a in range(TPG):
+                        nc.tensor.transpose(tp[:, a, :], raw[:, a, c0 : c0 + E].bitcast(F32), ident_f[:])
+                    nc.scalar.copy(out=dst[:, h * GROUP : (h + 1) * GROUP], in_=tp[:].rearrange("p a r -> p (a r)"))
+            vg = vgp.tile([P, H * E, 4], BF16, name="vg", align_bytes=64)
+            nc.gpsimd.tensor_scalar(
+                out=vg[:],
+                in0=raw[:, :, 2 * H * E : 3 * H * E].rearrange("p t c -> p c t"),
+                scalar1=1.0,
+                scalar2=0.0,
+                op0=ALU.mult,
+                op1=ALU.add,
+            )
+            nc.vector.quantize_mx(
+                out=vcodes[:, g, :].bitcast(FP8X4),
+                scales=vscales[:, g, :],
+                in_=vg[:].rearrange("p c t -> p (c t)"),
+            )
+
+        def halves(ap2d):
+            return ap2d.bitcast(BF16).rearrange("p (r e) -> p r e", e=2)
+
+        def step(i):
+            g, a = divmod(i, TPG)
+            lo = 0 if g > 0 else (TPG - a)
+            n_prev = (TPG - a) if g > 0 else 0
+            tmp = work.tile([P, H, WIN], F32, name="tmp")
+            for h in range(H):
+                qv = halves(qts[g][:, h * GROUP + a * P : h * GROUP + (a + 1) * P])
+                parts = []
+                if g > 0:
+                    parts.append((kts[g - 1], a, TPG, 0))
+                parts.append((kts[g], 0, a + 1, TPG - a))
+                for kt, t0, t1, s0 in parts:
+                    n = (t1 - t0) * P
+                    kv = halves(kt[:, h * GROUP + t0 * P : h * GROUP + t1 * P])
+                    sp = ps_s.tile([P, GROUP], F32, name="sp", tag="s")
+                    for ee in range(2):
+                        nc.tensor.matmul(sp[:, :n], lhsT=qv[:, :, ee], rhs=kv[:, :, ee], start=(ee == 0), stop=(ee == 1))
+                    nc.vector.scalar_tensor_tensor(
+                        out=tmp[:, h, s0 * P : s0 * P + n],
+                        in0=sp[:, :n],
+                        scalar=1.0 / 16.0,
+                        in1=btab[:, h, s0 * P : s0 * P + n],
+                        op0=ALU.mult,
+                        op1=ALU.add,
+                    )
+            negm = small.tile([P, H], F32, name="negm")
+            nc.vector.tensor_reduce(out=negm[:], in_=tmp[:, :, lo * P : WIN], axis=AX.X, op=ALU.max, negate=True)
+            rsum = small.tile([P, H], F32, name="rsum")
+            ee_t = work.tile([P, H, WIN], BF16, name="ee_t")
+            for h in range(H):
+                nc.scalar.activation(
+                    out=ee_t[:, h, lo * P : WIN],
+                    in_=tmp[:, h, lo * P : WIN],
+                    func=ACTF.Exp,
+                    bias=negm[:, h : h + 1],
+                    scale=1.0,
+                    accum_out=rsum[:, h : h + 1],
+                )
+            recip = small.tile([P, H], F32, name="recip")
+            nc.vector.reciprocal(out=recip[:], in_=rsum[:])
+            gv = grouped[a][:].rearrange("p (h g q t) -> p h g q t", h=H, g=2, q=P, t=4)
+            ets = work.tile([P, H, SLOTS, P], BF16, name="ets")
+            for h in range(H):
+                et = ps_t.tile([P, SLOTS, P], BF16, name="et", tag="T")
+                for s in range(lo, SLOTS):
+                    nc.tensor.transpose(et[:, s, :], ee_t[:, h, s * P : (s + 1) * P], ident_b[:])
+                nc.scalar.copy(out=ets[:, h, lo:SLOTS, :], in_=et[:, lo:SLOTS, :])
+            if g > 0:
+                nc.gpsimd.tensor_scalar(
+                    out=gv[:, :, 0, :, a:4],
+                    in0=ets[:, :, 0:n_prev, :].rearrange("p h s q -> p h q s"),
+                    scalar1=1.0,
+                    scalar2=0.0,
+                    op0=ALU.mult,
+                    op1=ALU.add,
+                )
+            nc.gpsimd.tensor_scalar(
+                out=gv[:, :, 1, :, 0 : a + 1],
+                in0=ets[:, :, TPG - a : SLOTS, :].rearrange("p h s q -> p h q s"),
+                scalar1=1.0,
+                scalar2=0.0,
+                op0=ALU.mult,
+                op1=ALU.add,
+            )
+            codes = work.tile([P, H * 2 * P], U32, name="codes", align_bytes=64)
+            scales = work.tile([P, H * 2 * P], U8, name="scales", align_bytes=64)
+            nc.vector.quantize_mx(out=codes[:].bitcast(FP8X4), scales=scales[:], in_=grouped[a][:])
+            osb = work.tile([P, H, E], F32, name="osb")
+            for h in range(H):
+                po = ps_o.tile([P, E], F32, name="po", tag="o")
+                passes = [(1, g)] if g == 0 else [(0, g - 1), (1, g)]
+                for n_p, (grp, gg) in enumerate(passes):
+                    c0 = (h * 2 + grp) * P
+                    nc.tensor.matmul_mx(
+                        out=po[:],
+                        lhsT=codes[:, c0 : c0 + P].bitcast(FP8X4),
+                        lhsT_scale=scales[:, c0 : c0 + P],
+                        rhs=vcodes[:, gg, h * E : (h + 1) * E].bitcast(FP8X4),
+                        rhs_scale=vscales[:, gg, h * E : (h + 1) * E],
+                        start=(n_p == 0),
+                        stop=(n_p == len(passes) - 1),
+                    )
+                nc.scalar.activation(out=osb[:, h, :], in_=po[:], func=ACTF.Copy, scale=recip[:, h : h + 1])
+            nc.sync.dma_start(out=y[i * P : (i + 1) * P, :], in_=osb[:].rearrange("p h e -> p (h e)"))
+
+        prep(0)
+        for g in range(NG):
+            for a in range(TPG):
+                if a == 1 and g + 1 < NG:
+                    prep(g + 1)
+                step(g * TPG + a)

@@ -41,8 +41,9 @@ def tile_flexattention_t_kernel(tc, qkv, out):
         qtp = ctx.enter_context(tc.tile_pool(name="qtp", bufs=2))
         ktp = ctx.enter_context(tc.tile_pool(name="ktp", bufs=3))
         vgp = ctx.enter_context(tc.tile_pool(name="vgp", bufs=2))
-        work = ctx.enter_context(tc.tile_pool(name="work", bufs=4))
-        small = ctx.enter_context(tc.tile_pool(name="small", bufs=4))
+        work = ctx.enter_context(tc.tile_pool(name="work", bufs=3))
+        ctx.enter_context(tc.manual_schedule())
+        small = ctx.enter_context(tc.tile_pool(name="small", bufs=8))
         ps_s = ctx.enter_context(tc.psum_pool(name="ps_s", bufs=4))
         ps_t = ctx.enter_context(tc.psum_pool(name="ps_t", bufs=2))
         ps_o = ctx.enter_context(tc.psum_pool(name="ps_o", bufs=2))
@@ -75,110 +76,131 @@ def tile_flexattention_t_kernel(tc, qkv, out):
             nc.vector.memset(gr[:], 0.0)
             grouped.append(gr)
 
-        qts = {}
-        kts = {}
+        NT = L // P
+        raws, qts, kts, vgs = {}, {}, {}, {}
+        tmps, negms, ees, rsums, recips, etss, codess, scaless = {}, {}, {}, {}, {}, {}, {}, {}
 
-        def prep(g):
+        def load(g):
             raw = rawp.tile([P, TPG, ROW], BF16, name="raw")
+            raws[g] = raw
             for a in range(TPG):
                 r0 = g * GROUP + a * P
                 nc.sync.dma_start(out=raw[:, a, :], in_=x[r0 : r0 + P, :])
-            qt = qtp.tile([P, H * GROUP], F32, name="qt")
-            kt = ktp.tile([P, H * GROUP], F32, name="kt")
-            qts[g] = qt
-            kts[g] = kt
-            for w, dst in ((1, kt), (0, qt)):
-                for h in range(H):
-                    tp = ps_t.tile([P, TPG, P], F32, name="tp", tag="T")
-                    c0 = (w * H + h) * E
-                    for a in range(TPG):
-                        nc.tensor.transpose(tp[:, a, :], raw[:, a, c0 : c0 + E].bitcast(F32), ident_f[:])
-                    nc.scalar.copy(out=dst[:, h * GROUP : (h + 1) * GROUP], in_=tp[:].rearrange("p a r -> p (a r)"))
+
+        def flip(g, b):
+            w, h = (1, b) if b < 2 else (0, b - 2)
+            if b == 0:
+                kts[g] = ktp.tile([P, H * GROUP], F32, name="kt")
+            if b == 2:
+                qts[g] = qtp.tile([P, H * GROUP], F32, name="qt")
+            dst = kts[g] if w == 1 else qts[g]
+            tp = ps_t.tile([P, TPG, P], F32, name="tp", tag="T")
+            c0 = (w * H + h) * E
+            for a in range(TPG):
+                nc.tensor.transpose(tp[:, a, :], raws[g][:, a, c0 : c0 + E].bitcast(F32), ident_f[:])
+            nc.scalar.copy(out=dst[:, h * GROUP : (h + 1) * GROUP], in_=tp[:].rearrange("p a r -> p (a r)"))
+
+        def v_regroup(g):
             vg = vgp.tile([P, H * E, 4], BF16, name="vg", align_bytes=64)
+            vgs[g] = vg
             nc.gpsimd.tensor_scalar(
-                out=vg[:],
-                in0=raw[:, :, 2 * H * E : 3 * H * E].rearrange("p t c -> p c t"),
-                scalar1=1.0,
-                scalar2=0.0,
-                op0=ALU.mult,
-                op1=ALU.add,
+                out=vg[:], in0=raws[g][:, :, 2 * H * E : 3 * H * E].rearrange("p t c -> p c t"),
+                scalar1=1.0, scalar2=0.0, op0=ALU.mult, op1=ALU.add,
             )
+
+        def v_quant(g):
             nc.vector.quantize_mx(
-                out=vcodes[:, g, :].bitcast(FP8X4),
-                scales=vscales[:, g, :],
-                in_=vg[:].rearrange("p c t -> p (c t)"),
+                out=vcodes[:, g, :].bitcast(FP8X4), scales=vscales[:, g, :], in_=vgs[g][:].rearrange("p c t -> p (c t)")
             )
 
         def halves(ap2d):
             return ap2d.bitcast(BF16).rearrange("p (r e) -> p r e", e=2)
 
-        def step(i):
+        def live(i):
             g, a = divmod(i, TPG)
-            lo = 0 if g > 0 else (TPG - a)
-            n_prev = (TPG - a) if g > 0 else 0
-            tmp = work.tile([P, H, WIN], F32, name="tmp")
-            for h in range(H):
-                qv = halves(qts[g][:, h * GROUP + a * P : h * GROUP + (a + 1) * P])
-                parts = []
-                if g > 0:
-                    parts.append((kts[g - 1], a, TPG, 0))
-                parts.append((kts[g], 0, a + 1, TPG - a))
-                for kt, t0, t1, s0 in parts:
-                    n = (t1 - t0) * P
-                    kv = halves(kt[:, h * GROUP + t0 * P : h * GROUP + t1 * P])
-                    sp = ps_s.tile([P, GROUP], F32, name="sp", tag="s")
-                    for ee in range(2):
-                        nc.tensor.matmul(sp[:, :n], lhsT=qv[:, :, ee], rhs=kv[:, :, ee], start=(ee == 0), stop=(ee == 1))
-                    nc.vector.scalar_tensor_tensor(
-                        out=tmp[:, h, s0 * P : s0 * P + n],
-                        in0=sp[:, :n],
-                        scalar=1.0 / 16.0,
-                        in1=btab[:, h, s0 * P : s0 * P + n],
-                        op0=ALU.mult,
-                        op1=ALU.add,
-                    )
-            negm = small.tile([P, H], F32, name="negm")
-            nc.vector.tensor_reduce(out=negm[:], in_=tmp[:, :, lo * P : WIN], axis=AX.X, op=ALU.max, negate=True)
-            rsum = small.tile([P, H], F32, name="rsum")
-            ee_t = work.tile([P, H, WIN], BF16, name="ee_t")
+            return g, a, (0 if g > 0 else TPG - a)
+
+        def qk(i, h, part):
+            g, a, lo = live(i)
+            if not (0 <= i < NT) or (part == 0 and g == 0):
+                return
+            if i not in tmps:
+                tmps[i] = work.tile([P, H, WIN], F32, name="tmp")
+            kt, t0, t1, s0 = (kts[g - 1], a, TPG, 0) if part == 0 else (kts[g], 0, a + 1, TPG - a)
+            n = (t1 - t0) * P
+            qv = halves(qts[g][:, h * GROUP + a * P : h * GROUP + (a + 1) * P])
+            kv = halves(kt[:, h * GROUP + t0 * P : h * GROUP + t1 * P])
+            sp = ps_s.tile([P, GROUP], F32, name="sp", tag="s")
+            for ee in range(2):
+                nc.tensor.matmul(sp[:, :n], lhsT=qv[:, :, ee], rhs=kv[:, :, ee], start=(ee == 0), stop=(ee == 1))
+            nc.vector.scalar_tensor_tensor(
+                out=tmps[i][:, h, s0 * P : s0 * P + n], in0=sp[:, :n], scalar=1.0 / 16.0,
+                in1=btab[:, h, s0 * P : s0 * P + n], op0=ALU.mult, op1=ALU.add,
+            )
+
+        def rowmax(i):
+            if not (0 <= i < NT):
+                return
+            g, a, lo = live(i)
+            negms[i] = small.tile([P, H], F32, name="negm")
+            nc.vector.tensor_reduce(out=negms[i][:], in_=tmps[i][:, :, lo * P : WIN], axis=AX.X, op=ALU.max, negate=True)
+
+        def expo(i):
+            if not (0 <= i < NT):
+                return
+            g, a, lo = live(i)
+            rsums[i] = small.tile([P, H], F32, name="rsum")
+            ees[i] = work.tile([P, H, WIN], BF16, name="ee_t")
             for h in range(H):
                 nc.scalar.activation(
-                    out=ee_t[:, h, lo * P : WIN],
-                    in_=tmp[:, h, lo * P : WIN],
-                    func=ACTF.Exp,
-                    bias=negm[:, h : h + 1],
-                    scale=1.0,
-                    accum_out=rsum[:, h : h + 1],
+                    out=ees[i][:, h, lo * P : WIN], in_=tmps[i][:, h, lo * P : WIN], func=ACTF.Exp,
+                    bias=negms[i][:, h : h + 1], scale=1.0, accum_out=rsums[i][:, h : h + 1],
                 )
-            recip = small.tile([P, H], F32, name="recip")
-            nc.vector.reciprocal(out=recip[:], in_=rsum[:])
+
+        def recipro(i):
+            if not (0 <= i < NT):
+                return
+            recips[i] = small.tile([P, H], F32, name="recip")
+            nc.vector.reciprocal(out=recips[i][:], in_=rsums[i][:])
+
+        def flip_e(i, h):
+            if not (0 <= i < NT):
+                return
+            g, a, lo = live(i)
+            if h == 0:
+                etss[i] = work.tile([P, H, SLOTS, P], BF16, name="ets")
+            et = ps_t.tile([P, SLOTS, P], BF16, name="et", tag="T")
+            for s in range(lo, SLOTS):
+                nc.tensor.transpose(et[:, s, :], ees[i][:, h, s * P : (s + 1) * P], ident_b[:])
+            nc.scalar.copy(out=etss[i][:, h, lo:SLOTS, :], in_=et[:, lo:SLOTS, :])
+
+        def regroup(i):
+            if not (0 <= i < NT):
+                return
+            g, a, lo = live(i)
             gv = grouped[a][:].rearrange("p (h g q t) -> p h g q t", h=H, g=2, q=P, t=4)
-            ets = work.tile([P, H, SLOTS, P], BF16, name="ets")
-            for h in range(H):
-                et = ps_t.tile([P, SLOTS, P], BF16, name="et", tag="T")
-                for s in range(lo, SLOTS):
-                    nc.tensor.transpose(et[:, s, :], ee_t[:, h, s * P : (s + 1) * P], ident_b[:])
-                nc.scalar.copy(out=ets[:, h, lo:SLOTS, :], in_=et[:, lo:SLOTS, :])
             if g > 0:
                 nc.gpsimd.tensor_scalar(
-                    out=gv[:, :, 0, :, a:4],
-                    in0=ets[:, :, 0:n_prev, :].rearrange("p h s q -> p h q s"),
-                    scalar1=1.0,
-                    scalar2=0.0,
-                    op0=ALU.mult,
-                    op1=ALU.add,
+                    out=gv[:, :, 0, :, a:4], in0=etss[i][:, :, 0 : TPG - a, :].rearrange("p h s q -> p h q s"),
+                    scalar1=1.0, scalar2=0.0, op0=ALU.mult, op1=ALU.add,
                 )
             nc.gpsimd.tensor_scalar(
-                out=gv[:, :, 1, :, 0 : a + 1],
-                in0=ets[:, :, TPG - a : SLOTS, :].rearrange("p h s q -> p h q s"),
-                scalar1=1.0,
-                scalar2=0.0,
-                op0=ALU.mult,
-                op1=ALU.add,
+                out=gv[:, :, 1, :, 0 : a + 1], in0=etss[i][:, :, TPG - a : SLOTS, :].rearrange("p h s q -> p h q s"),
+                scalar1=1.0, scalar2=0.0, op0=ALU.mult, op1=ALU.add,
             )
-            codes = work.tile([P, H * 2 * P], U32, name="codes", align_bytes=64)
-            scales = work.tile([P, H * 2 * P], U8, name="scales", align_bytes=64)
-            nc.vector.quantize_mx(out=codes[:].bitcast(FP8X4), scales=scales[:], in_=grouped[a][:])
+
+        def quant(i):
+            if not (0 <= i < NT):
+                return
+            g, a, lo = live(i)
+            codess[i] = work.tile([P, H * 2 * P], U32, name="codes", align_bytes=64)
+            scaless[i] = work.tile([P, H * 2 * P], U8, name="scales", align_bytes=64)
+            nc.vector.quantize_mx(out=codess[i][:].bitcast(FP8X4), scales=scaless[i][:], in_=grouped[a][:])
+
+        def pv(i):
+            if not (0 <= i < NT):
+                return
+            g, a, lo = live(i)
             osb = work.tile([P, H, E], F32, name="osb")
             for h in range(H):
                 po = ps_o.tile([P, E], F32, name="po", tag="o")
@@ -186,20 +208,39 @@ def tile_flexattention_t_kernel(tc, qkv, out):
                 for n_p, (grp, gg) in enumerate(passes):
                     c0 = (h * 2 + grp) * P
                     nc.tensor.matmul_mx(
-                        out=po[:],
-                        lhsT=codes[:, c0 : c0 + P].bitcast(FP8X4),
-                        lhsT_scale=scales[:, c0 : c0 + P],
-                        rhs=vcodes[:, gg, h * E : (h + 1) * E].bitcast(FP8X4),
-                        rhs_scale=vscales[:, gg, h * E : (h + 1) * E],
-                        start=(n_p == 0),
-                        stop=(n_p == len(passes) - 1),
+                        out=po[:], lhsT=codess[i][:, c0 : c0 + P].bitcast(FP8X4), lhsT_scale=scaless[i][:, c0 : c0 + P],
+                        rhs=vcodes[:, gg, h * E : (h + 1) * E].bitcast(FP8X4), rhs_scale=vscales[:, gg, h * E : (h + 1) * E],
+                        start=(n_p == 0), stop=(n_p == len(passes) - 1),
                     )
-                nc.scalar.activation(out=osb[:, h, :], in_=po[:], func=ACTF.Copy, scale=recip[:, h : h + 1])
+                nc.scalar.activation(out=osb[:, h, :], in_=po[:], func=ACTF.Copy, scale=recips[i][:, h : h + 1])
             nc.sync.dma_start(out=y[i * P : (i + 1) * P, :], in_=osb[:].rearrange("p h e -> p (h e)"))
 
-        prep(0)
-        for g in range(NG):
-            for a in range(TPG):
-                if a == 1 and g + 1 < NG:
-                    prep(g + 1)
-                step(g * TPG + a)
+        load(0)
+        load(1)
+        for b in range(4):
+            flip(0, b)
+        v_regroup(0)
+        v_quant(0)
+        for n in range(NT + 5):
+            g_next = n // TPG + 1
+            b = n % TPG
+            flip_e(n - 2, 0)
+            flip_e(n - 2, 1)
+            qk(n, 0, 0)
+            qk(n, 0, 1)
+            if g_next < NG:
+                flip(g_next, b)
+            expo(n - 1)
+            quant(n - 4)
+            recipro(n - 2)
+            if g_next < NG and b == 2:
+                v_quant(g_next)
+            qk(n, 1, 0)
+            pv(n - 5)
+            qk(n, 1, 1)
+            rowmax(n)
+            regroup(n - 3)
+            if g_next < NG and b == 0:
+                v_regroup(g_next)
+            if b == 0 and g_next + 1 < NG:
+                load(g_next + 1)

@@ -134,8 +134,8 @@ def tile_flexattention_t_kernel(tc, qkv, out):
             for ee in range(2):
                 nc.tensor.matmul(sp[:, :n], lhsT=qv[:, :, ee], rhs=kv[:, :, ee], start=(ee == 0), stop=(ee == 1))
             nc.vector.scalar_tensor_tensor(
-                out=tmps[i][:, h, s0 * P : s0 * P + n], in0=sp[:, :n], scalar=1.0 / 16.0,
-                in1=btab[:, h, s0 * P : s0 * P + n], op0=ALU.mult, op1=ALU.add,
+                out=tmps[i][:, h, s0 * P : s0 * P + n], in0=sp[:, :n], scalar=-1.0 / 16.0,
+                in1=btab[:, h, s0 * P : s0 * P + n], op0=ALU.mult, op1=ALU.subtract,
             )
 
         def rowmax(i):
@@ -143,7 +143,11 @@ def tile_flexattention_t_kernel(tc, qkv, out):
                 return
             g, a, lo = live(i)
             negms[i] = small.tile([P, H], F32, name="negm")
-            nc.vector.tensor_reduce(out=negms[i][:], in_=tmps[i][:, :, lo * P : WIN], axis=AX.X, op=ALU.max, negate=True)
+            for h in range(H):
+                nc.vector.tensor_scalar(
+                    out=tmps[i][:, h, lo * P : WIN], in0=tmps[i][:, h, lo * P : WIN], scalar1=1.0, scalar2=None,
+                    op0=ALU.mult, op1=ALU.min, accum_out=negms[i][:, h : h + 1],
+                )
 
         def expo(i):
             if not (0 <= i < NT):
@@ -154,7 +158,7 @@ def tile_flexattention_t_kernel(tc, qkv, out):
             for h in range(H):
                 nc.scalar.activation(
                     out=ees[i][:, h, lo * P : WIN], in_=tmps[i][:, h, lo * P : WIN], func=ACTF.Exp,
-                    bias=negms[i][:, h : h + 1], scale=1.0, accum_out=rsums[i][:, h : h + 1],
+                    bias=negms[i][:, h : h + 1], scale=-1.0, accum_out=rsums[i][:, h : h + 1],
                 )
 
         def recipro(i):
@@ -180,13 +184,11 @@ def tile_flexattention_t_kernel(tc, qkv, out):
             g, a, lo = live(i)
             gv = grouped[a][:].rearrange("p (h g q t) -> p h g q t", h=H, g=2, q=P, t=4)
             if g > 0:
-                nc.gpsimd.tensor_scalar(
-                    out=gv[:, :, 0, :, a:4], in0=etss[i][:, :, 0 : TPG - a, :].rearrange("p h s q -> p h q s"),
-                    scalar1=1.0, scalar2=0.0, op0=ALU.mult, op1=ALU.add,
+                nc.vector.tensor_copy(
+                    out=gv[:, :, 0, :, a:4], in_=etss[i][:, :, 0 : TPG - a, :].rearrange("p h s q -> p h q s")
                 )
-            nc.gpsimd.tensor_scalar(
-                out=gv[:, :, 1, :, 0 : a + 1], in0=etss[i][:, :, TPG - a : SLOTS, :].rearrange("p h s q -> p h q s"),
-                scalar1=1.0, scalar2=0.0, op0=ALU.mult, op1=ALU.add,
+            nc.vector.tensor_copy(
+                out=gv[:, :, 1, :, 0 : a + 1], in_=etss[i][:, :, TPG - a : SLOTS, :].rearrange("p h s q -> p h q s")
             )
 
         def quant(i):
@@ -232,6 +234,7 @@ def tile_flexattention_t_kernel(tc, qkv, out):
                 flip(g_next, b)
             expo(n - 1)
             quant(n - 4)
+            regroup(n - 3)
             recipro(n - 2)
             if g_next < NG and b == 2:
                 v_quant(g_next)
@@ -239,7 +242,6 @@ def tile_flexattention_t_kernel(tc, qkv, out):
             pv(n - 5)
             qk(n, 1, 1)
             rowmax(n)
-            regroup(n - 3)
             if g_next < NG and b == 0:
                 v_regroup(g_next)
             if b == 0 and g_next + 1 < NG:

@@ -45,16 +45,15 @@ def tile_flexattention_t_kernel(tc, qkv, out):
         ctx.enter_context(tc.manual_schedule())
         small = ctx.enter_context(tc.tile_pool(name="small", bufs=8))
         ps_s = ctx.enter_context(tc.psum_pool(name="ps_s", bufs=4))
-        ps_t = ctx.enter_context(tc.psum_pool(name="ps_t", bufs=2))
-        ps_o = ctx.enter_context(tc.psum_pool(name="ps_o", bufs=2))
+        ps_t = ctx.enter_context(tc.psum_pool(name="ps_t", bufs=1))
+        ps_o = ctx.enter_context(tc.psum_pool(name="ps_o", bufs=1))
 
+        dist_i = const.tile([P, WIN], I32, name="dist_i")
+        nc.gpsimd.iota(dist_i[:], pattern=[[-1, WIN]], base=GROUP, channel_multiplier=1)
         ident_f = const.tile([P, P], F32, name="ident_f")
         make_identity(nc, ident_f[:])
         ident_b = const.tile([P, P], BF16, name="ident_b")
         make_identity(nc, ident_b[:])
-
-        dist_i = const.tile([P, WIN], I32, name="dist_i")
-        nc.gpsimd.iota(dist_i[:], pattern=[[-1, WIN]], base=GROUP, channel_multiplier=1)
         dist = const.tile([P, WIN], F32, name="dist")
         nc.vector.tensor_copy(out=dist[:], in_=dist_i[:])
         pen_a = const.tile([P, WIN], F32, name="pen_a")
@@ -73,7 +72,7 @@ def tile_flexattention_t_kernel(tc, qkv, out):
         grouped = []
         for a in range(TPG):
             gr = const.tile([P, H * 2 * P * 4], BF16, name="gr%d" % a, align_bytes=64)
-            nc.vector.memset(gr[:], 0.0)
+            nc.gpsimd.memset(gr[:], 0.0)
             grouped.append(gr)
 
         NT = L // P
@@ -94,11 +93,16 @@ def tile_flexattention_t_kernel(tc, qkv, out):
             if b == 2:
                 qts[g] = qtp.tile([P, H * GROUP], F32, name="qt")
             dst = kts[g] if w == 1 else qts[g]
-            tp = ps_t.tile([P, TPG, P], F32, name="tp", tag="T")
+            tp = ps_t.tile([P, TPG, P], F32, name="tp", tag="T2")
             c0 = (w * H + h) * E
-            for a in range(TPG):
+
+            def one(a):
                 nc.tensor.transpose(tp[:, a, :], raws[g][:, a, c0 : c0 + E].bitcast(F32), ident_f[:])
-            nc.scalar.copy(out=dst[:, h * GROUP : (h + 1) * GROUP], in_=tp[:].rearrange("p a r -> p (a r)"))
+
+            def fin():
+                nc.scalar.copy(out=dst[:, h * GROUP : (h + 1) * GROUP], in_=tp[:].rearrange("p a r -> p (a r)"))
+
+            return [(one, a) for a in range(TPG)], fin
 
         def v_regroup(g):
             vg = vgp.tile([P, H * E, 4], BF16, name="vg", align_bytes=64)
@@ -120,7 +124,17 @@ def tile_flexattention_t_kernel(tc, qkv, out):
             g, a = divmod(i, TPG)
             return g, a, (0 if g > 0 else TPG - a)
 
-        def qk(i, h, part):
+        def queue(items):
+            return {"items": items, "at": 0}
+
+        def pop(todo, k):
+            for unused in range(k):
+                if todo["at"] < len(todo["items"]):
+                    f, arg = todo["items"][todo["at"]]
+                    todo["at"] = todo["at"] + 1
+                    f(arg)
+
+        def qk(i, h, part, todo):
             g, a, lo = live(i)
             if not (0 <= i < NT) or (part == 0 and g == 0):
                 return
@@ -133,9 +147,10 @@ def tile_flexattention_t_kernel(tc, qkv, out):
             sp = ps_s.tile([P, GROUP], F32, name="sp", tag="s")
             for ee in range(2):
                 nc.tensor.matmul(sp[:, :n], lhsT=qv[:, :, ee], rhs=kv[:, :, ee], start=(ee == 0), stop=(ee == 1))
+                pop(todo, 2)
             nc.vector.scalar_tensor_tensor(
-                out=tmps[i][:, h, s0 * P : s0 * P + n], in0=sp[:, :n], scalar=-1.0 / 16.0,
-                in1=btab[:, h, s0 * P : s0 * P + n], op0=ALU.mult, op1=ALU.subtract,
+                out=tmps[i][:, h, s0 * P : s0 * P + n], in0=sp[:, :n], scalar=1.0 / 16.0,
+                in1=btab[:, h, s0 * P : s0 * P + n], op0=ALU.mult, op1=ALU.add,
             )
 
         def rowmax(i):
@@ -143,11 +158,7 @@ def tile_flexattention_t_kernel(tc, qkv, out):
                 return
             g, a, lo = live(i)
             negms[i] = small.tile([P, H], F32, name="negm")
-            for h in range(H):
-                nc.vector.tensor_scalar(
-                    out=tmps[i][:, h, lo * P : WIN], in0=tmps[i][:, h, lo * P : WIN], scalar1=1.0, scalar2=None,
-                    op0=ALU.mult, op1=ALU.min, accum_out=negms[i][:, h : h + 1],
-                )
+            nc.vector.tensor_reduce(out=negms[i][:], in_=tmps[i][:, :, lo * P : WIN], axis=AX.X, op=ALU.max, negate=True)
 
         def expo(i):
             if not (0 <= i < NT):
@@ -158,7 +169,7 @@ def tile_flexattention_t_kernel(tc, qkv, out):
             for h in range(H):
                 nc.scalar.activation(
                     out=ees[i][:, h, lo * P : WIN], in_=tmps[i][:, h, lo * P : WIN], func=ACTF.Exp,
-                    bias=negms[i][:, h : h + 1], scale=-1.0, accum_out=rsums[i][:, h : h + 1],
+                    bias=negms[i][:, h : h + 1], scale=1.0, accum_out=rsums[i][:, h : h + 1],
                 )
 
         def recipro(i):
@@ -169,14 +180,19 @@ def tile_flexattention_t_kernel(tc, qkv, out):
 
         def flip_e(i, h):
             if not (0 <= i < NT):
-                return
+                return [], None
             g, a, lo = live(i)
             if h == 0:
                 etss[i] = work.tile([P, H, SLOTS, P], BF16, name="ets")
-            et = ps_t.tile([P, SLOTS, P], BF16, name="et", tag="T")
-            for s in range(lo, SLOTS):
+            et = ps_t.tile([P, SLOTS, P], BF16, name="et", tag="T%d" % h)
+
+            def one(s):
                 nc.tensor.transpose(et[:, s, :], ees[i][:, h, s * P : (s + 1) * P], ident_b[:])
-            nc.scalar.copy(out=etss[i][:, h, lo:SLOTS, :], in_=et[:, lo:SLOTS, :])
+
+            def fin():
+                nc.scalar.copy(out=etss[i][:, h, lo:SLOTS, :], in_=et[:, lo:SLOTS, :])
+
+            return [(one, s) for s in range(lo, SLOTS)], fin
 
         def regroup(i):
             if not (0 <= i < NT):
@@ -184,11 +200,13 @@ def tile_flexattention_t_kernel(tc, qkv, out):
             g, a, lo = live(i)
             gv = grouped[a][:].rearrange("p (h g q t) -> p h g q t", h=H, g=2, q=P, t=4)
             if g > 0:
-                nc.vector.tensor_copy(
-                    out=gv[:, :, 0, :, a:4], in_=etss[i][:, :, 0 : TPG - a, :].rearrange("p h s q -> p h q s")
+                nc.gpsimd.tensor_scalar(
+                    out=gv[:, :, 0, :, a:4], in0=etss[i][:, :, 0 : TPG - a, :].rearrange("p h s q -> p h q s"),
+                    scalar1=1.0, scalar2=0.0, op0=ALU.mult, op1=ALU.add,
                 )
-            nc.vector.tensor_copy(
-                out=gv[:, :, 1, :, 0 : a + 1], in_=etss[i][:, :, TPG - a : SLOTS, :].rearrange("p h s q -> p h q s")
+            nc.gpsimd.tensor_scalar(
+                out=gv[:, :, 1, :, 0 : a + 1], in0=etss[i][:, :, TPG - a : SLOTS, :].rearrange("p h s q -> p h q s"),
+                scalar1=1.0, scalar2=0.0, op0=ALU.mult, op1=ALU.add,
             )
 
         def quant(i):
@@ -199,49 +217,73 @@ def tile_flexattention_t_kernel(tc, qkv, out):
             scaless[i] = work.tile([P, H * 2 * P], U8, name="scales", align_bytes=64)
             nc.vector.quantize_mx(out=codess[i][:].bitcast(FP8X4), scales=scaless[i][:], in_=grouped[a][:])
 
+        pos = {}
+
         def pv(i):
             if not (0 <= i < NT):
                 return
             g, a, lo = live(i)
-            osb = work.tile([P, H, E], F32, name="osb")
+            po = ps_o.tile([P, H, E], F32, name="po", tag="o")
+            pos[i] = po
             for h in range(H):
-                po = ps_o.tile([P, E], F32, name="po", tag="o")
                 passes = [(1, g)] if g == 0 else [(0, g - 1), (1, g)]
                 for n_p, (grp, gg) in enumerate(passes):
                     c0 = (h * 2 + grp) * P
                     nc.tensor.matmul_mx(
-                        out=po[:], lhsT=codess[i][:, c0 : c0 + P].bitcast(FP8X4), lhsT_scale=scaless[i][:, c0 : c0 + P],
+                        out=po[:, h, :], lhsT=codess[i][:, c0 : c0 + P].bitcast(FP8X4), lhsT_scale=scaless[i][:, c0 : c0 + P],
                         rhs=vcodes[:, gg, h * E : (h + 1) * E].bitcast(FP8X4), rhs_scale=vscales[:, gg, h * E : (h + 1) * E],
                         start=(n_p == 0), stop=(n_p == len(passes) - 1),
                     )
-                nc.scalar.activation(out=osb[:, h, :], in_=po[:], func=ACTF.Copy, scale=recips[i][:, h : h + 1])
+
+        def finish(i):
+            if not (0 <= i < NT):
+                return
+            osb = work.tile([P, H, E], F32, name="osb")
+            if i % 2 == 0:
+                nc.vector.tensor_tensor(
+                    out=osb[:], in0=pos[i][:], in1=recips[i][:].unsqueeze(2).to_broadcast([P, H, E]), op=ALU.mult
+                )
+            else:
+                for h in (1, 0):
+                    nc.scalar.activation(out=osb[:, h, :], in_=pos[i][:, h, :], func=ACTF.Copy, scale=recips[i][:, h : h + 1])
             nc.sync.dma_start(out=y[i * P : (i + 1) * P, :], in_=osb[:].rearrange("p h e -> p (h e)"))
 
         load(0)
         load(1)
-        for b in range(4):
-            flip(0, b)
+        for b in (0, 2, 1, 3):
+            items, fin = flip(0, b)
+            pop(queue(items), TPG)
+            fin()
         v_regroup(0)
         v_quant(0)
         for n in range(NT + 5):
             g_next = n // TPG + 1
             b = n % TPG
-            flip_e(n - 2, 0)
-            flip_e(n - 2, 1)
-            qk(n, 0, 0)
-            qk(n, 0, 1)
-            if g_next < NG:
-                flip(g_next, b)
             expo(n - 1)
+            t0, fin0 = flip_e(n - 2, 0)
+            t1, fin1 = flip_e(n - 2, 1)
+            todo = queue(t0 + t1)
+            qk(n, 0, 0, todo)
+            qk(n, 0, 1, todo)
             quant(n - 4)
-            regroup(n - 3)
             recipro(n - 2)
             if g_next < NG and b == 2:
                 v_quant(g_next)
-            qk(n, 1, 0)
+            qk(n, 1, 0, todo)
+            pop(todo, 2 * SLOTS)
+            if fin0 is not None:
+                fin0()
+                fin1()
             pv(n - 5)
-            qk(n, 1, 1)
+            items, fin = flip(g_next, b) if g_next < NG else ([], None)
+            todo = queue(items)
+            qk(n, 1, 1, todo)
+            pop(todo, TPG)
+            if fin is not None:
+                fin()
+            finish(n - 5)
             rowmax(n)
+            regroup(n - 3)
             if g_next < NG and b == 0:
                 v_regroup(g_next)
             if b == 0 and g_next + 1 < NG:

@@ -69,14 +69,14 @@ def tile_flexattention_t_kernel(tc, qkv, out):
 
         vcodes = const.tile([P, NG, H * E], U32, name="vcodes", align_bytes=64)
         vscales = const.tile([P, NG, H * E], U8, name="vscales", align_bytes=64)
-        grouped = []
+        etp = []
         for a in range(TPG):
-            gr = const.tile([P, H * 2 * P * 4], BF16, name="gr%d" % a, align_bytes=64)
-            nc.gpsimd.memset(gr[:], 0.0)
-            grouped.append(gr)
+            ets = const.tile([P, H * 2 * TPG * P], BF16, name="ets%d" % a)
+            nc.gpsimd.memset(ets[:], 0.0)
+            etp.append(ets)
 
         NT = L // P
-        raws, qts, kts, vgs = {}, {}, {}, {}
+        raws, qts, kts, vgs, grs = {}, {}, {}, {}, {}
         tmps, negms, ees, rsums, recips, etss, codess, scaless = {}, {}, {}, {}, {}, {}, {}, {}
 
         def load(g):
@@ -107,9 +107,9 @@ def tile_flexattention_t_kernel(tc, qkv, out):
         def v_regroup(g):
             vg = vgp.tile([P, H * E, 4], BF16, name="vg", align_bytes=64)
             vgs[g] = vg
-            nc.gpsimd.tensor_scalar(
-                out=vg[:], in0=raws[g][:, :, 2 * H * E : 3 * H * E].rearrange("p t c -> p c t"),
-                scalar1=1.0, scalar2=0.0, op0=ALU.mult, op1=ALU.add,
+            nc.scalar.copy(
+                out=vg[:].rearrange("p (c i) t -> p c t i", i=4),
+                in_=raws[g][:, :, 2 * H * E : 3 * H * E].rearrange("p t (c i) -> p c t i", i=4),
             )
 
         def v_quant(g):
@@ -182,15 +182,14 @@ def tile_flexattention_t_kernel(tc, qkv, out):
             if not (0 <= i < NT):
                 return [], None
             g, a, lo = live(i)
-            if h == 0:
-                etss[i] = work.tile([P, H, SLOTS, P], BF16, name="ets")
+            etv = etp[a][:].rearrange("p (h s q) -> p h s q", h=H, s=2 * TPG, q=P)
             et = ps_t.tile([P, SLOTS, P], BF16, name="et", tag="T%d" % h)
 
             def one(s):
                 nc.tensor.transpose(et[:, s, :], ees[i][:, h, s * P : (s + 1) * P], ident_b[:])
 
             def fin():
-                nc.scalar.copy(out=etss[i][:, h, lo:SLOTS, :], in_=et[:, lo:SLOTS, :])
+                nc.scalar.copy(out=etv[:, h, a + lo : a + SLOTS, :], in_=et[:, lo:SLOTS, :])
 
             return [(one, s) for s in range(lo, SLOTS)], fin
 
@@ -198,14 +197,10 @@ def tile_flexattention_t_kernel(tc, qkv, out):
             if not (0 <= i < NT):
                 return
             g, a, lo = live(i)
-            gv = grouped[a][:].rearrange("p (h g q t) -> p h g q t", h=H, g=2, q=P, t=4)
-            if g > 0:
-                nc.gpsimd.tensor_scalar(
-                    out=gv[:, :, 0, :, a:4], in0=etss[i][:, :, 0 : TPG - a, :].rearrange("p h s q -> p h q s"),
-                    scalar1=1.0, scalar2=0.0, op0=ALU.mult, op1=ALU.add,
-                )
+            grs[i] = work.tile([P, H * 2 * P * 4], BF16, name="gr", align_bytes=64)
             nc.gpsimd.tensor_scalar(
-                out=gv[:, :, 1, :, 0 : a + 1], in0=etss[i][:, :, TPG - a : SLOTS, :].rearrange("p h s q -> p h q s"),
+                out=grs[i][:].rearrange("p (u q t) -> p u q t", u=2 * H, q=P, t=4),
+                in0=etp[a][:].rearrange("p (u t q) -> p u q t", u=2 * H, t=4, q=P),
                 scalar1=1.0, scalar2=0.0, op0=ALU.mult, op1=ALU.add,
             )
 
@@ -215,7 +210,7 @@ def tile_flexattention_t_kernel(tc, qkv, out):
             g, a, lo = live(i)
             codess[i] = work.tile([P, H * 2 * P], U32, name="codes", align_bytes=64)
             scaless[i] = work.tile([P, H * 2 * P], U8, name="scales", align_bytes=64)
-            nc.vector.quantize_mx(out=codess[i][:].bitcast(FP8X4), scales=scaless[i][:], in_=grouped[a][:])
+            nc.vector.quantize_mx(out=codess[i][:].bitcast(FP8X4), scales=scaless[i][:], in_=grs[i][:])
 
         pos = {}
 
@@ -239,7 +234,7 @@ def tile_flexattention_t_kernel(tc, qkv, out):
             if not (0 <= i < NT):
                 return
             osb = work.tile([P, H, E], F32, name="osb")
-            if i % 2 == 0:
+            if i % 4 == 0:
                 nc.vector.tensor_tensor(
                     out=osb[:], in0=pos[i][:], in1=recips[i][:].unsqueeze(2).to_broadcast([P, H, E]), op=ALU.mult
                 )

@@ -69,14 +69,14 @@ def tile_flexattention_t_kernel(tc, qkv, out):
 
         vcodes = const.tile([P, NG, H * E], U32, name="vcodes", align_bytes=64)
         vscales = const.tile([P, NG, H * E], U8, name="vscales", align_bytes=64)
-        etp = []
+        grouped = []
         for a in range(TPG):
-            ets = const.tile([P, H * 2 * TPG * P], BF16, name="ets%d" % a)
-            nc.gpsimd.memset(ets[:], 0.0)
-            etp.append(ets)
+            gr = const.tile([P, H * 2 * P * 4], BF16, name="gr%d" % a, align_bytes=64)
+            nc.gpsimd.memset(gr[:], 0.0)
+            grouped.append(gr)
 
         NT = L // P
-        raws, qts, kts, vgs, grs = {}, {}, {}, {}, {}
+        raws, qts, kts, vgs = {}, {}, {}, {}
         tmps, negms, ees, rsums, recips, etss, codess, scaless = {}, {}, {}, {}, {}, {}, {}, {}
 
         def load(g):
@@ -104,13 +104,23 @@ def tile_flexattention_t_kernel(tc, qkv, out):
 
             return [(one, a) for a in range(TPG)], fin
 
-        def v_regroup(g):
-            vg = vgp.tile([P, H * E, 4], BF16, name="vg", align_bytes=64)
-            vgs[g] = vg
+        def v_regroup(g, j):
+            if j == 0:
+                vgs[g] = vgp.tile([P, H * E, 4], BF16, name="vg", align_bytes=64)
+            c0 = j * P
             nc.scalar.copy(
-                out=vg[:].rearrange("p (c i) t -> p c t i", i=4),
-                in_=raws[g][:, :, 2 * H * E : 3 * H * E].rearrange("p t (c i) -> p c t i", i=4),
+                out=vgs[g][:, c0 : c0 + P, :].rearrange("p (c i) t -> p c t i", i=4),
+                in_=raws[g][:, :, 2 * H * E + c0 : 2 * H * E + c0 + P].rearrange("p t (c i) -> p c t i", i=4),
             )
+
+        def flip_first(a):
+            tp = ps_t.tile([P, TPG, P], F32, name="tp", tag="T2")
+            for j, c0 in enumerate((2 * E, 3 * E, 0, E)):
+                nc.tensor.transpose(tp[:, j, :], raws[0][:, a, c0 : c0 + E].bitcast(F32), ident_f[:])
+            for j, dst in ((0, kts[0]), (2, qts[0])):
+                nc.scalar.copy(
+                    out=dst[:].rearrange("p (h a r) -> p h a r", h=H, a=TPG)[:, :, a, :], in_=tp[:, j : j + 2, :]
+                )
 
         def v_quant(g):
             nc.vector.quantize_mx(
@@ -182,14 +192,15 @@ def tile_flexattention_t_kernel(tc, qkv, out):
             if not (0 <= i < NT):
                 return [], None
             g, a, lo = live(i)
-            etv = etp[a][:].rearrange("p (h s q) -> p h s q", h=H, s=2 * TPG, q=P)
+            if h == 0:
+                etss[i] = work.tile([P, H, SLOTS, P], BF16, name="ets")
             et = ps_t.tile([P, SLOTS, P], BF16, name="et", tag="T%d" % h)
 
             def one(s):
                 nc.tensor.transpose(et[:, s, :], ees[i][:, h, s * P : (s + 1) * P], ident_b[:])
 
             def fin():
-                nc.scalar.copy(out=etv[:, h, a + lo : a + SLOTS, :], in_=et[:, lo:SLOTS, :])
+                nc.scalar.copy(out=etss[i][:, h, lo:SLOTS, :], in_=et[:, lo:SLOTS, :])
 
             return [(one, s) for s in range(lo, SLOTS)], fin
 
@@ -197,10 +208,22 @@ def tile_flexattention_t_kernel(tc, qkv, out):
             if not (0 <= i < NT):
                 return
             g, a, lo = live(i)
-            grs[i] = work.tile([P, H * 2 * P * 4], BF16, name="gr", align_bytes=64)
+            gv = grouped[a][:].rearrange("p (h g q t) -> p h g q t", h=H, g=2, q=P, t=4)
+            if i >= NT - 3:
+                nc.vector.tensor_copy(
+                    out=gv[:, :, 0, :, a:4], in_=etss[i][:, :, 0 : TPG - a, :].rearrange("p h s q -> p h q s")
+                )
+                nc.vector.tensor_copy(
+                    out=gv[:, :, 1, :, 0 : a + 1], in_=etss[i][:, :, TPG - a : SLOTS, :].rearrange("p h s q -> p h q s")
+                )
+                return
+            if g > 0:
+                nc.gpsimd.tensor_scalar(
+                    out=gv[:, :, 0, :, a:4], in0=etss[i][:, :, 0 : TPG - a, :].rearrange("p h s q -> p h q s"),
+                    scalar1=1.0, scalar2=0.0, op0=ALU.mult, op1=ALU.add,
+                )
             nc.gpsimd.tensor_scalar(
-                out=grs[i][:].rearrange("p (u q t) -> p u q t", u=2 * H, q=P, t=4),
-                in0=etp[a][:].rearrange("p (u t q) -> p u q t", u=2 * H, t=4, q=P),
+                out=gv[:, :, 1, :, 0 : a + 1], in0=etss[i][:, :, TPG - a : SLOTS, :].rearrange("p h s q -> p h q s"),
                 scalar1=1.0, scalar2=0.0, op0=ALU.mult, op1=ALU.add,
             )
 
@@ -210,7 +233,7 @@ def tile_flexattention_t_kernel(tc, qkv, out):
             g, a, lo = live(i)
             codess[i] = work.tile([P, H * 2 * P], U32, name="codes", align_bytes=64)
             scaless[i] = work.tile([P, H * 2 * P], U8, name="scales", align_bytes=64)
-            nc.vector.quantize_mx(out=codess[i][:].bitcast(FP8X4), scales=scaless[i][:], in_=grs[i][:])
+            nc.vector.quantize_mx(out=codess[i][:].bitcast(FP8X4), scales=scaless[i][:], in_=grouped[a][:])
 
         pos = {}
 
@@ -245,12 +268,9 @@ def tile_flexattention_t_kernel(tc, qkv, out):
 
         load(0)
         load(1)
-        for b in (0, 2, 1, 3):
-            items, fin = flip(0, b)
-            pop(queue(items), TPG)
-            fin()
-        v_regroup(0)
-        v_quant(0)
+        kts[0] = ktp.tile([P, H * GROUP], F32, name="kt")
+        qts[0] = qtp.tile([P, H * GROUP], F32, name="qt")
+        flip_first(0)
         for n in range(NT + 5):
             g_next = n // TPG + 1
             b = n % TPG
@@ -262,8 +282,10 @@ def tile_flexattention_t_kernel(tc, qkv, out):
             qk(n, 0, 1, todo)
             quant(n - 4)
             recipro(n - 2)
-            if g_next < NG and b == 2:
-                v_quant(g_next)
+            if n == 2:
+                v_quant(0)
+            if b == 0 and 0 < n < NT:
+                v_quant(n // TPG)
             qk(n, 1, 0, todo)
             pop(todo, 2 * SLOTS)
             if fin0 is not None:
@@ -276,10 +298,15 @@ def tile_flexattention_t_kernel(tc, qkv, out):
             pop(todo, TPG)
             if fin is not None:
                 fin()
+            if n + 1 < TPG:
+                flip_first(n + 1)
             finish(n - 5)
+            if n < 2:
+                v_regroup(0, 2 * n)
+                v_regroup(0, 2 * n + 1)
+            if g_next < NG:
+                v_regroup(g_next, b)
             rowmax(n)
             regroup(n - 3)
-            if g_next < NG and b == 0:
-                v_regroup(g_next)
             if b == 0 and g_next + 1 < NG:
                 load(g_next + 1)

@@ -21,12 +21,15 @@ H = 2
 E = 256
 GROUP = 512
 NG = L // GROUP
+NT = L // P
 TPG = GROUP // P
 SLOTS = TPG + 1
 WIN = SLOTS * P
-ROW = 3 * H * E
-BIG = 30000.0
+MAIN = 3 * P
+HE = H * E
+BIG = 2.0 ** 40
 SLOPES = (2.0 ** -4, 2.0 ** -8)
+QK_AHEAD = 8
 
 FLOPS = 2 * 2 * E * H * (GROUP * GROUP + (NG - 1) * GROUP * 2 * GROUP)
 
@@ -37,216 +40,281 @@ def tile_flexattention_t_kernel(tc, qkv, out):
     y = out.rearrange("b l h e -> (b l) (h e)")
     with ExitStack() as ctx:
         const = ctx.enter_context(tc.tile_pool(name="const", bufs=1))
-        rawp = ctx.enter_context(tc.tile_pool(name="rawp", bufs=3))
-        qtp = ctx.enter_context(tc.tile_pool(name="qtp", bufs=2))
-        ktp = ctx.enter_context(tc.tile_pool(name="ktp", bufs=3))
+        rawp = ctx.enter_context(tc.tile_pool(name="rawp", bufs=QK_AHEAD))
+        rawvp = ctx.enter_context(tc.tile_pool(name="rawvp", bufs=3))
         vgp = ctx.enter_context(tc.tile_pool(name="vgp", bufs=2))
         work = ctx.enter_context(tc.tile_pool(name="work", bufs=3))
         ctx.enter_context(tc.manual_schedule())
         small = ctx.enter_context(tc.tile_pool(name="small", bufs=8))
-        ps_s = ctx.enter_context(tc.psum_pool(name="ps_s", bufs=4))
-        ps_t = ctx.enter_context(tc.psum_pool(name="ps_t", bufs=1))
-        ps_o = ctx.enter_context(tc.psum_pool(name="ps_o", bufs=1))
+        ps_s = ctx.enter_context(tc.psum_pool(name="ps_s", bufs=5))
+        ps_w = ctx.enter_context(tc.psum_pool(name="ps_w", bufs=2))
+        ps_y = ctx.enter_context(tc.psum_pool(name="ps_y", bufs=1))
 
-        dist_i = const.tile([P, WIN], I32, name="dist_i")
-        nc.gpsimd.iota(dist_i[:], pattern=[[-1, WIN]], base=GROUP, channel_multiplier=1)
-        ident_f = const.tile([P, P], F32, name="ident_f")
-        make_identity(nc, ident_f[:])
-        ident_b = const.tile([P, P], BF16, name="ident_b")
-        make_identity(nc, ident_b[:])
-        dist = const.tile([P, WIN], F32, name="dist")
-        nc.vector.tensor_copy(out=dist[:], in_=dist_i[:])
-        pen_a = const.tile([P, WIN], F32, name="pen_a")
-        nc.vector.tensor_scalar(out=pen_a[:], in0=dist[:], scalar1=0.0, scalar2=-BIG, op0=ALU.is_lt, op1=ALU.mult)
-        pen_b = const.tile([P, WIN], F32, name="pen_b")
-        nc.vector.tensor_scalar(out=pen_b[:], in0=dist[:], scalar1=float(GROUP), scalar2=-BIG, op0=ALU.is_ge, op1=ALU.mult)
-        nc.vector.tensor_tensor(out=pen_a[:], in0=pen_a[:], in1=pen_b[:], op=ALU.add)
-        btab = const.tile([P, H, WIN], F32, name="btab")
-        for h in range(H):
-            nc.vector.scalar_tensor_tensor(
-                out=btab[:, h, :], in0=dist[:], scalar=-SLOPES[h], in1=pen_a[:], op0=ALU.mult, op1=ALU.add
-            )
+        raws, rawvs, vgs = {}, {}, {}
 
-        vcodes = const.tile([P, NG, H * E], U32, name="vcodes", align_bytes=64)
-        vscales = const.tile([P, NG, H * E], U8, name="vscales", align_bytes=64)
-        grouped = []
-        for a in range(TPG):
-            gr = const.tile([P, H * 2 * P * 4], BF16, name="gr%d" % a, align_bytes=64)
-            nc.gpsimd.memset(gr[:], 0.0)
-            grouped.append(gr)
+        def load_qk(i):
+            if i >= NT:
+                return
+            raw = rawp.tile([P, 2 * HE], BF16, name="raw")
+            raws[i] = raw
+            nc.sync.dma_start(out=raw[:], in_=x[i * P : (i + 1) * P, 0 : 2 * HE])
 
-        NT = L // P
-        raws, qts, kts, vgs = {}, {}, {}, {}
-        tmps, negms, ees, rsums, recips, etss, codess, scaless = {}, {}, {}, {}, {}, {}, {}, {}
-
-        def load(g):
-            raw = rawp.tile([P, TPG, ROW], BF16, name="raw")
-            raws[g] = raw
-            for a in range(TPG):
-                r0 = g * GROUP + a * P
-                nc.sync.dma_start(out=raw[:, a, :], in_=x[r0 : r0 + P, :])
-
-        def flip(g, b):
-            w, h = (1, b) if b < 2 else (0, b - 2)
-            if b == 0:
-                kts[g] = ktp.tile([P, H * GROUP], F32, name="kt")
-            if b == 2:
-                qts[g] = qtp.tile([P, H * GROUP], F32, name="qt")
-            dst = kts[g] if w == 1 else qts[g]
-            tp = ps_t.tile([P, TPG, P], F32, name="tp", tag="T2")
-            c0 = (w * H + h) * E
-
-            def one(a):
-                nc.tensor.transpose(tp[:, a, :], raws[g][:, a, c0 : c0 + E].bitcast(F32), ident_f[:])
-
-            def fin():
-                nc.scalar.copy(out=dst[:, h * GROUP : (h + 1) * GROUP], in_=tp[:].rearrange("p a r -> p (a r)"))
-
-            return [(one, a) for a in range(TPG)], fin
-
-        def v_regroup(g, j):
-            if j == 0:
-                vgs[g] = vgp.tile([P, H * E, 4], BF16, name="vg", align_bytes=64)
-            c0 = j * P
-            nc.scalar.copy(
-                out=vgs[g][:, c0 : c0 + P, :].rearrange("p (c i) t -> p c t i", i=4),
-                in_=raws[g][:, :, 2 * H * E + c0 : 2 * H * E + c0 + P].rearrange("p t (c i) -> p c t i", i=4),
-            )
-
-        def flip_first(a):
-            tp = ps_t.tile([P, TPG, P], F32, name="tp", tag="T2")
-            for j, c0 in enumerate((2 * E, 3 * E, 0, E)):
-                nc.tensor.transpose(tp[:, j, :], raws[0][:, a, c0 : c0 + E].bitcast(F32), ident_f[:])
-            for j, dst in ((0, kts[0]), (2, qts[0])):
-                nc.scalar.copy(
-                    out=dst[:].rearrange("p (h a r) -> p h a r", h=H, a=TPG)[:, :, a, :], in_=tp[:, j : j + 2, :]
+        def load_v(g):
+            if g >= NG:
+                return
+            rv = rawvp.tile([P, 4, HE], BF16, name="rv")
+            rawvs[g] = rv
+            for u in range(2):
+                r0 = g * GROUP + u * 2 * P
+                nc.sync.dma_start(
+                    out=rv[:, 2 * u : 2 * u + 2, :],
+                    in_=x[r0 : r0 + 2 * P, 2 * HE : 3 * HE].rearrange("(p e) c -> p e c", e=2),
                 )
 
-        def v_quant(g):
-            nc.vector.quantize_mx(
-                out=vcodes[:, g, :].bitcast(FP8X4), scales=vscales[:, g, :], in_=vgs[g][:].rearrange("p c t -> p (c t)")
+        load_qk(0)
+        load_qk(1)
+        load_qk(2)
+        load_v(0)
+        for i in range(3, QK_AHEAD):
+            load_qk(i)
+        load_v(1)
+
+        ident_f = const.tile([P, P], F32, name="ident_f")
+        make_identity(nc, ident_f[:])
+        dist_i = const.tile([P, WIN], I32, name="dist_i")
+        nc.gpsimd.iota(dist_i[:], pattern=[[1, WIN]], base=-2 * P, channel_multiplier=-1)
+        ident_b = const.tile([P, P], BF16, name="ident_b")
+        make_identity(nc, ident_b[:])
+        zero = const.tile([P, P], F32, name="zero")
+        nc.vector.memset(zero[:], 0.0)
+        warm = const.tile([P, 1], F32, name="warm")
+        nc.scalar.activation(out=warm[:], in_=zero[:, 0:1], func=ACTF.Exp)
+        dist = const.tile([P, WIN], F32, name="dist")
+        nc.vector.tensor_copy(out=dist[:], in_=dist_i[:])
+        pen = const.tile([P, 2, P], F32, name="pen")
+        nc.vector.tensor_scalar(
+            out=pen[:, 0, :], in0=dist[:, 0:P], scalar1=-256.0, scalar2=-BIG, op0=ALU.is_le, op1=ALU.mult
+        )
+        nc.vector.tensor_scalar(
+            out=pen[:, 1, :], in0=dist[:, WIN - P : WIN], scalar1=256.0, scalar2=-BIG, op0=ALU.is_gt, op1=ALU.mult
+        )
+        tab_tri = const.tile([P, H, 2, P], BF16, name="tab_tri")
+        tab_main = const.tile([P, H, MAIN], BF16, name="tab_main")
+        for h in range(H):
+            nc.vector.scalar_tensor_tensor(
+                out=tab_tri[:, h, :, :], in0=dist[:].rearrange("p (s c) -> p s c", s=SLOTS)[:, 0 : SLOTS : SLOTS - 1, :],
+                scalar=16.0 * SLOPES[h], in1=pen[:], op0=ALU.mult, op1=ALU.add,
+            )
+            nc.vector.tensor_scalar(
+                out=tab_main[:, h, :], in0=dist[:, P : P + MAIN], scalar1=16.0 * SLOPES[h], scalar2=None, op0=ALU.mult
             )
 
-        def halves(ap2d):
-            return ap2d.bitcast(BF16).rearrange("p (r e) -> p r e", e=2)
+        qkt = const.tile([P, 2 * H, L], F32, name="qkt")
+        vcodes = const.tile([P, NG, HE], U32, name="vcodes", align_bytes=64)
+        vscales = const.tile([P, NG, HE], U8, name="vscales", align_bytes=64)
+        ebuf = []
+        for k in range(4):
+            eb = const.tile([P, H, 6 * P], BF16, name="eb%d" % k)
+            ebuf.append(eb)
+            pad = 5 * P if k % 2 == 0 else 0
+            nc.vector.memset(eb[:, :, pad : pad + P], 0.0)
+        yt = ps_y.tile([P, 2 * H, P], F32, name="yt", tag="y")
+        for b in range(H):
+            nc.tensor.transpose(yt[:, 2 * b + 1, :], zero[:], ident_f[:])
 
         def live(i):
             g, a = divmod(i, TPG)
-            return g, a, (0 if g > 0 else TPG - a)
+            return g, a, (max(1, TPG - i))
 
-        def queue(items):
-            return {"items": items, "at": 0}
+        tps, tris, mains = {}, {}, {}
+        mxs, negms, rss, rsums, recips = {}, {}, {}, {}, {}
+        xts, grs, codess, scaless, pos = {}, {}, {}, {}, {}
 
-        def pop(todo, k):
-            for unused in range(k):
-                if todo["at"] < len(todo["items"]):
-                    f, arg = todo["items"][todo["at"]]
-                    todo["at"] = todo["at"] + 1
-                    f(arg)
+        def ok(i):
+            return 0 <= i < NT
 
-        def qk(i, h, part, todo):
-            g, a, lo = live(i)
-            if not (0 <= i < NT) or (part == 0 and g == 0):
+        def flip_qk(i):
+            if not ok(i):
                 return
-            if i not in tmps:
-                tmps[i] = work.tile([P, H, WIN], F32, name="tmp")
-            kt, t0, t1, s0 = (kts[g - 1], a, TPG, 0) if part == 0 else (kts[g], 0, a + 1, TPG - a)
-            n = (t1 - t0) * P
-            qv = halves(qts[g][:, h * GROUP + a * P : h * GROUP + (a + 1) * P])
-            kv = halves(kt[:, h * GROUP + t0 * P : h * GROUP + t1 * P])
-            sp = ps_s.tile([P, GROUP], F32, name="sp", tag="s")
-            for ee in range(2):
-                nc.tensor.matmul(sp[:, :n], lhsT=qv[:, :, ee], rhs=kv[:, :, ee], start=(ee == 0), stop=(ee == 1))
-                pop(todo, 2)
-            nc.vector.scalar_tensor_tensor(
-                out=tmps[i][:, h, s0 * P : s0 * P + n], in0=sp[:, :n], scalar=1.0 / 16.0,
-                in1=btab[:, h, s0 * P : s0 * P + n], op0=ALU.mult, op1=ALU.add,
+            tp = ps_w.tile([P, 2 * H, P], F32, name="tp", tag="w")
+            tps[i] = tp
+            for j in range(2 * H):
+                nc.tensor.transpose(tp[:, j, :], raws[i][:, j * E : (j + 1) * E].bitcast(F32), ident_f[:])
+
+        def evac_qk(i):
+            if not ok(i):
+                return
+            nc.scalar.copy(out=qkt[:, :, i * P : (i + 1) * P], in_=tps[i][:])
+
+        def q_half(i, h, ee):
+            return qkt[:, h, i * P : (i + 1) * P].bitcast(BF16).rearrange("p (r e) -> p r e", e=2)[:, :, ee]
+
+        def score_tri(i):
+            if not ok(i):
+                return
+            st = ps_s.tile([P, H, 2, P], F32, name="st", tag="s")
+            tris[i] = st
+            nc.tensor.matmul(
+                st[:].rearrange("p h s c -> p (h s c)"), lhsT=ident_b[:], rhs=tab_tri[:].rearrange("p h s c -> p (h s c)"),
+                start=True, stop=False,
             )
-
-        def rowmax(i):
-            if not (0 <= i < NT):
-                return
-            g, a, lo = live(i)
-            negms[i] = small.tile([P, H], F32, name="negm")
-            nc.vector.tensor_reduce(out=negms[i][:], in_=tmps[i][:, :, lo * P : WIN], axis=AX.X, op=ALU.max, negate=True)
-
-        def expo(i):
-            if not (0 <= i < NT):
-                return
-            g, a, lo = live(i)
-            rsums[i] = small.tile([P, H], F32, name="rsum")
-            ees[i] = work.tile([P, H, WIN], BF16, name="ee_t")
             for h in range(H):
-                nc.scalar.activation(
-                    out=ees[i][:, h, lo * P : WIN], in_=tmps[i][:, h, lo * P : WIN], func=ACTF.Exp,
-                    bias=negms[i][:, h : h + 1], scale=1.0, accum_out=rsums[i][:, h : h + 1],
+                for ee in range(2):
+                    last = h == H - 1 and ee == 1
+                    if i >= TPG:
+                        kv = qkt[:, H + h, (i - TPG) * P : (i + 1) * P].bitcast(BF16)
+                        kv = kv.rearrange("p (s r e) -> p s r e", s=SLOTS, e=2)[:, 0 : SLOTS : SLOTS - 1, :, ee]
+                        nc.tensor.matmul(st[:, h, :, :], lhsT=q_half(i, h, ee), rhs=kv, start=False, stop=last)
+                    else:
+                        nc.tensor.matmul(
+                            st[:, h, 1, :], lhsT=q_half(i, h, ee), rhs=q_half(i, H + h, ee), start=False, stop=last
+                        )
+
+        def score_main(i, h):
+            if not ok(i) or i == 0:
+                return
+            g, a, lo = live(i)
+            mt = ps_s.tile([P, MAIN], F32, name="mt", tag="s")
+            mains[i, h] = mt
+            c0 = (lo - 1) * P
+            nc.tensor.matmul(mt[:, c0:MAIN], lhsT=ident_b[:], rhs=tab_main[:, h, c0:MAIN], start=True, stop=False)
+            kv = qkt[:, H + h, (i - TPG + lo) * P : i * P].bitcast(BF16).rearrange("p (r e) -> p r e", e=2)
+            for ee in range(2):
+                nc.tensor.matmul(mt[:, c0:MAIN], lhsT=q_half(i, h, ee), rhs=kv[:, :, ee], start=False, stop=(ee == 1))
+
+        def max_tri(i):
+            if not ok(i):
+                return
+            mxs[i] = small.tile([P, 2 * H], F32, name="mx")
+            negms[i] = small.tile([P, H], F32, name="negm")
+            s0 = 0 if i >= TPG else 1
+            nc.vector.tensor_reduce(
+                out=mxs[i][:, 0:H], in_=tris[i][:, :, s0:2, :].rearrange("p h s c -> p h (s c)"), axis=AX.X, op=ALU.max, negate=True
+            )
+            if i == 0:
+                nc.vector.tensor_scalar(
+                    out=negms[i][:], in0=mxs[i][:, 0:H], scalar1=1.0 / 16.0, scalar2=None, op0=ALU.mult
                 )
 
-        def recipro(i):
-            if not (0 <= i < NT):
+        def max_main(i, h):
+            if not ok(i) or i == 0:
                 return
-            recips[i] = small.tile([P, H], F32, name="recip")
-            nc.vector.reciprocal(out=recips[i][:], in_=rsums[i][:])
+            g, a, lo = live(i)
+            nc.vector.tensor_reduce(
+                out=mxs[i][:, H + h : H + h + 1], in_=mains[i, h][:, (lo - 1) * P : MAIN], axis=AX.X, op=ALU.max, negate=True
+            )
 
-        def flip_e(i, h):
-            if not (0 <= i < NT):
-                return [], None
+        def comb(i, h):
+            if not ok(i) or i == 0:
+                return
+            nc.vector.tensor_scalar(
+                out=negms[i][:, h : h + 1], in0=mxs[i][:, h : h + 1], scalar1=mxs[i][:, H + h : H + h + 1],
+                scalar2=1.0 / 16.0, op0=ALU.min, op1=ALU.mult,
+            )
+
+        def expo(i, h):
+            if not ok(i):
+                return
             g, a, lo = live(i)
             if h == 0:
-                etss[i] = work.tile([P, H, SLOTS, P], BF16, name="ets")
-            et = ps_t.tile([P, SLOTS, P], BF16, name="et", tag="T%d" % h)
-
-            def one(s):
-                nc.tensor.transpose(et[:, s, :], ees[i][:, h, s * P : (s + 1) * P], ident_b[:])
-
-            def fin():
-                nc.scalar.copy(out=etss[i][:, h, lo:SLOTS, :], in_=et[:, lo:SLOTS, :])
-
-            return [(one, s) for s in range(lo, SLOTS)], fin
-
-        def regroup(i):
-            if not (0 <= i < NT):
-                return
-            g, a, lo = live(i)
-            gv = grouped[a][:].rearrange("p (h g q t) -> p h g q t", h=H, g=2, q=P, t=4)
-            if i >= NT - 3:
-                nc.vector.tensor_copy(
-                    out=gv[:, :, 0, :, a:4], in_=etss[i][:, :, 0 : TPG - a, :].rearrange("p h s q -> p h q s")
-                )
-                nc.vector.tensor_copy(
-                    out=gv[:, :, 1, :, 0 : a + 1], in_=etss[i][:, :, TPG - a : SLOTS, :].rearrange("p h s q -> p h q s")
-                )
-                return
-            if g > 0:
-                nc.gpsimd.tensor_scalar(
-                    out=gv[:, :, 0, :, a:4], in0=etss[i][:, :, 0 : TPG - a, :].rearrange("p h s q -> p h q s"),
-                    scalar1=1.0, scalar2=0.0, op0=ALU.mult, op1=ALU.add,
-                )
-            nc.gpsimd.tensor_scalar(
-                out=gv[:, :, 1, :, 0 : a + 1], in0=etss[i][:, :, TPG - a : SLOTS, :].rearrange("p h s q -> p h q s"),
-                scalar1=1.0, scalar2=0.0, op0=ALU.mult, op1=ALU.add,
+                rss[i] = small.tile([P, 2 * H], F32, name="rs")
+            eb = ebuf[i % 4]
+            base = 0 if i % 2 == 0 else P
+            ev = eb[:, h, base : base + WIN].rearrange("p (s c) -> p s c", s=SLOTS)
+            s0 = 0 if i >= TPG else 1
+            nc.scalar.activation(
+                out=ev[:, s0 * (SLOTS - 1) : SLOTS : SLOTS - 1, :], in_=tris[i][:, h, s0:2, :], func=ACTF.Exp,
+                bias=negms[i][:, h : h + 1], scale=1.0 / 16.0, accum_out=rss[i][:, h : h + 1],
             )
+            if i > 0:
+                nc.scalar.activation(
+                    out=eb[:, h, base + lo * P : base + TPG * P], in_=mains[i, h][:, (lo - 1) * P : MAIN], func=ACTF.Exp,
+                    bias=negms[i][:, h : h + 1], scale=1.0 / 16.0, accum_out=rss[i][:, H + h : H + h + 1],
+                )
+
+        def rsum(i):
+            if not ok(i):
+                return
+            if i == 0:
+                rsums[i] = rss[i]
+                return
+            rsums[i] = small.tile([P, H], F32, name="rsum")
+            nc.gpsimd.tensor_tensor(out=rsums[i][:], in0=rss[i][:, 0:H], in1=rss[i][:, H : 2 * H], op=ALU.add)
+
+        def recipro(i):
+            if not ok(i):
+                return
+            recips[i] = small.tile([P, H], F32, name="recip")
+            nc.vector.reciprocal(out=recips[i][:], in_=rsums[i][:, 0:H])
+
+        def kind(i):
+            g, a = divmod(i, TPG)
+            early = a < 2
+            xw, yw = ((0, 1), 2) if early else ((1, 2), 0)
+            xs, ys = (0, 1) if early else (1, 0)
+            has_x = g > 0 or not early
+            has_y = g > 0 or early
+            return early, xw, yw, xs, ys, has_x, has_y
+
+        def word_block(i, h, j):
+            return ebuf[i % 4][:, h, 2 * P * j : 2 * P * (j + 1)].bitcast(F32)
+
+        def flip_e(i):
+            if not ok(i):
+                return
+            early, xw, yw, xs, ys, has_x, has_y = kind(i)
+            if has_x:
+                xt = ps_w.tile([P, 2 * H, P], F32, name="xt", tag="w")
+                xts[i] = xt
+                for h in range(H):
+                    for u in range(2):
+                        nc.tensor.transpose(xt[:, 2 * h + u, :], word_block(i, h, xw[u]), ident_f[:])
+            if has_y:
+                for h in range(H):
+                    nc.tensor.transpose(yt[:, 2 * h, :], word_block(i, h, yw), ident_f[:])
+
+        def gr_words(i, s):
+            if i not in grs:
+                grs[i] = work.tile([P, 2 * H * P * 4], BF16, name="gr", align_bytes=64)
+            return grs[i][:].bitcast(F32).rearrange("p (s h q u) -> p s h q u", s=2, h=H, q=P)[:, s, :, :, :]
+
+        def evac_x(i):
+            if not ok(i):
+                return
+            early, xw, yw, xs, ys, has_x, has_y = kind(i)
+            if has_x:
+                nc.scalar.copy(out=gr_words(i, xs), in_=xts[i][:].rearrange("p (h u) q -> p h q u", h=H))
+
+        def evac_y(i):
+            if not ok(i):
+                return
+            early, xw, yw, xs, ys, has_x, has_y = kind(i)
+            if has_y:
+                yv = yt[:].rearrange("p (h u) q -> p h u q", h=H)
+                if not early:
+                    yv = yv[:, :, ::-1, :]
+                nc.vector.tensor_copy(out=gr_words(i, ys), in_=yv.rearrange("p h u q -> p h q u"))
 
         def quant(i):
-            if not (0 <= i < NT):
+            if not ok(i):
                 return
-            g, a, lo = live(i)
-            codess[i] = work.tile([P, H * 2 * P], U32, name="codes", align_bytes=64)
-            scaless[i] = work.tile([P, H * 2 * P], U8, name="scales", align_bytes=64)
-            nc.vector.quantize_mx(out=codess[i][:].bitcast(FP8X4), scales=scaless[i][:], in_=grouped[a][:])
-
-        pos = {}
+            codess[i] = work.tile([P, 2 * H * P], U32, name="codes", align_bytes=64)
+            scaless[i] = work.tile([P, 2 * H * P], U8, name="scales", align_bytes=64)
+            c0 = 0 if i >= TPG else H * P
+            nc.vector.quantize_mx(
+                out=codess[i][:, c0:].bitcast(FP8X4), scales=scaless[i][:, c0:], in_=grs[i][:, 4 * c0 :]
+            )
 
         def pv(i):
-            if not (0 <= i < NT):
+            if not ok(i):
                 return
-            g, a, lo = live(i)
-            po = ps_o.tile([P, H, E], F32, name="po", tag="o")
+            g, a = divmod(i, TPG)
+            po = ps_w.tile([P, H, E], F32, name="po", tag="w")
             pos[i] = po
+            passes = [(1, g)] if g == 0 else [(0, g - 1), (1, g)]
             for h in range(H):
-                passes = [(1, g)] if g == 0 else [(0, g - 1), (1, g)]
-                for n_p, (grp, gg) in enumerate(passes):
-                    c0 = (h * 2 + grp) * P
+                for n_p, (s, gg) in enumerate(passes):
+                    c0 = (s * H + h) * P
                     nc.tensor.matmul_mx(
                         out=po[:, h, :], lhsT=codess[i][:, c0 : c0 + P].bitcast(FP8X4), lhsT_scale=scaless[i][:, c0 : c0 + P],
                         rhs=vcodes[:, gg, h * E : (h + 1) * E].bitcast(FP8X4), rhs_scale=vscales[:, gg, h * E : (h + 1) * E],
@@ -254,59 +322,64 @@ def tile_flexattention_t_kernel(tc, qkv, out):
                     )
 
         def finish(i):
-            if not (0 <= i < NT):
+            if not ok(i):
                 return
             osb = work.tile([P, H, E], F32, name="osb")
-            if i % 4 == 0:
+            if i % 3 == 0:
                 nc.vector.tensor_tensor(
                     out=osb[:], in0=pos[i][:], in1=recips[i][:].unsqueeze(2).to_broadcast([P, H, E]), op=ALU.mult
                 )
             else:
-                for h in (1, 0):
+                for h in range(H):
                     nc.scalar.activation(out=osb[:, h, :], in_=pos[i][:, h, :], func=ACTF.Copy, scale=recips[i][:, h : h + 1])
             nc.sync.dma_start(out=y[i * P : (i + 1) * P, :], in_=osb[:].rearrange("p h e -> p (h e)"))
 
-        load(0)
-        load(1)
-        kts[0] = ktp.tile([P, H * GROUP], F32, name="kt")
-        qts[0] = qtp.tile([P, H * GROUP], F32, name="qt")
-        flip_first(0)
-        for n in range(NT + 5):
-            g_next = n // TPG + 1
-            b = n % TPG
-            expo(n - 1)
-            t0, fin0 = flip_e(n - 2, 0)
-            t1, fin1 = flip_e(n - 2, 1)
-            todo = queue(t0 + t1)
-            qk(n, 0, 0, todo)
-            qk(n, 0, 1, todo)
-            quant(n - 4)
-            recipro(n - 2)
-            if n == 2:
-                v_quant(0)
-            if b == 0 and 0 < n < NT:
+        def v_regroup(g, j):
+            if g >= NG:
+                return
+            if j == 0:
+                vgs[g] = vgp.tile([P, HE, 4], BF16, name="vg", align_bytes=64)
+            c0 = j * P
+            nc.gpsimd.tensor_scalar(
+                out=vgs[g][:, c0 : c0 + P, :], in0=rawvs[g][:, :, c0 : c0 + P].rearrange("p t c -> p c t"),
+                scalar1=1.0, scalar2=0.0, op0=ALU.mult, op1=ALU.add,
+            )
+
+        def v_quant(g):
+            if g >= NG:
+                return
+            nc.vector.quantize_mx(
+                out=vcodes[:, g, :].bitcast(FP8X4), scales=vscales[:, g, :], in_=vgs[g][:].rearrange("p c t -> p (c t)")
+            )
+
+        flip_qk(0)
+        evac_qk(0)
+        for j in range(4):
+            v_regroup(0, j)
+        for n in range(NT + 3):
+            flip_e(n - 2)
+            flip_qk(n + 1)
+            max_main(n - 1, 1)
+            quant(n - 3)
+            comb(n - 1, 1)
+            expo(n - 1, 0)
+            evac_x(n - 2)
+            evac_y(n - 2)
+            score_tri(n)
+            score_main(n, 0)
+            max_tri(n)
+            max_main(n, 0)
+            recipro(n - 3)
+            comb(n, 0)
+            expo(n - 1, 1)
+            evac_qk(n + 1)
+            pv(n - 3)
+            score_main(n, 1)
+            finish(n - 3)
+            rsum(n - 1)
+            if n % TPG == 1:
                 v_quant(n // TPG)
-            qk(n, 1, 0, todo)
-            pop(todo, 2 * SLOTS)
-            if fin0 is not None:
-                fin0()
-                fin1()
-            pv(n - 5)
-            items, fin = flip(g_next, b) if g_next < NG else ([], None)
-            todo = queue(items)
-            qk(n, 1, 1, todo)
-            pop(todo, TPG)
-            if fin is not None:
-                fin()
-            if n + 1 < TPG:
-                flip_first(n + 1)
-            finish(n - 5)
-            if n < 2:
-                v_regroup(0, 2 * n)
-                v_regroup(0, 2 * n + 1)
-            if g_next < NG:
-                v_regroup(g_next, b)
-            rowmax(n)
-            regroup(n - 3)
-            if b == 0 and g_next + 1 < NG:
-                load(g_next + 1)
+            v_regroup(n // TPG + 1, n % TPG)
+            load_qk(n + QK_AHEAD)
+            if n % TPG == TPG - 1:
+                load_v(n // TPG + 2)

@@ -358,7 +358,6 @@ def tile_flexattention_t_kernel(tc, qkv, out):
             v_regroup(0, j)
         for n in range(NT + 3):
             flip_e(n - 2)
-            flip_qk(n + 1)
             max_main(n - 1, 1)
             quant(n - 3)
             comb(n - 1, 1)
@@ -366,12 +365,13 @@ def tile_flexattention_t_kernel(tc, qkv, out):
             evac_x(n - 2)
             evac_y(n - 2)
             score_tri(n)
+            flip_qk(n + 1)
             score_main(n, 0)
             max_tri(n)
-            max_main(n, 0)
             recipro(n - 3)
-            comb(n, 0)
+            max_main(n, 0)
             expo(n - 1, 1)
+            comb(n, 0)
             evac_qk(n + 1)
             pv(n - 3)
             score_main(n, 1)

@@ -325,7 +325,7 @@ def tile_flexattention_t_kernel(tc, qkv, out):
             if not ok(i):
                 return
             osb = work.tile([P, H, E], F32, name="osb")
-            if i % 3 == 0:
+            if i % 2 == 1:
                 nc.vector.tensor_tensor(
                     out=osb[:], in0=pos[i][:], in1=recips[i][:].unsqueeze(2).to_broadcast([P, H, E]), op=ALU.mult
                 )
@@ -352,8 +352,9 @@ def tile_flexattention_t_kernel(tc, qkv, out):
                 out=vcodes[:, g, :].bitcast(FP8X4), scales=vscales[:, g, :], in_=vgs[g][:].rearrange("p c t -> p (c t)")
             )
 
-        flip_qk(0)
-        evac_qk(0)
+        for i in range(1):
+            flip_qk(i)
+            evac_qk(i)
         for j in range(4):
             v_regroup(0, j)
         for n in range(NT + 3):
@@ -377,7 +378,7 @@ def tile_flexattention_t_kernel(tc, qkv, out):
             score_main(n, 1)
             finish(n - 3)
             rsum(n - 1)
-            if n % TPG == 1:
+            if n == 2 or (n > TPG and n % TPG == 1):
                 v_quant(n // TPG)
             v_regroup(n // TPG + 1, n % TPG)
             load_qk(n + QK_AHEAD)

@@ -325,7 +325,7 @@ def tile_flexattention_t_kernel(tc, qkv, out):
             if not ok(i):
                 return
             osb = work.tile([P, H, E], F32, name="osb")
-            if i % 2 == 1:
+            if i == NT - 1:
                 nc.vector.tensor_tensor(
                     out=osb[:], in0=pos[i][:], in1=recips[i][:].unsqueeze(2).to_broadcast([P, H, E]), op=ALU.mult
                 )

@@ -98,11 +98,12 @@ def tile_flexattention_t_kernel(tc, qkv, out):
         nc.vector.tensor_scalar(
             out=pen[:, 1, :], in0=dist[:, WIN - P : WIN], scalar1=256.0, scalar2=-BIG, op0=ALU.is_gt, op1=ALU.mult
         )
-        tab_tri = const.tile([P, H, 2, P], BF16, name="tab_tri")
+        tab_tri = const.tile([P, 2, P], BF16, name="tab_tri")
+        tab_tri1 = const.tile([P, 2, P], F32, name="tab_tri1")
         tab_main = const.tile([P, H, MAIN], BF16, name="tab_main")
         for h in range(H):
             nc.vector.scalar_tensor_tensor(
-                out=tab_tri[:, h, :, :], in0=dist[:].rearrange("p (s c) -> p s c", s=SLOTS)[:, 0 : SLOTS : SLOTS - 1, :],
+                out=(tab_tri if h == 0 else tab_tri1)[:], in0=dist[:].rearrange("p (s c) -> p s c", s=SLOTS)[:, 0 : SLOTS : SLOTS - 1, :],
                 scalar=16.0 * SLOPES[h], in1=pen[:], op0=ALU.mult, op1=ALU.add,
             )
             nc.vector.tensor_scalar(
@@ -128,6 +129,7 @@ def tile_flexattention_t_kernel(tc, qkv, out):
 
         tps, tris, mains = {}, {}, {}
         mxs, negms, rss, rsums, recips = {}, {}, {}, {}, {}
+        tms = {}
         xts, grs, codess, scaless, pos = {}, {}, {}, {}, {}
 
         def ok(i):
@@ -154,20 +156,22 @@ def tile_flexattention_t_kernel(tc, qkv, out):
                 return
             st = ps_s.tile([P, H, 2, P], F32, name="st", tag="s")
             tris[i] = st
-            nc.tensor.matmul(
-                st[:].rearrange("p h s c -> p (h s c)"), lhsT=ident_b[:], rhs=tab_tri[:].rearrange("p h s c -> p (h s c)"),
-                start=True, stop=False,
-            )
-            for h in range(H):
+            for h in (1, 0):
+                if h == 0:
+                    nc.tensor.matmul(
+                        st[:, h, :, :].rearrange("p s c -> p (s c)"), lhsT=ident_b[:],
+                        rhs=tab_tri[:].rearrange("p s c -> p (s c)"), start=True, stop=False,
+                    )
                 for ee in range(2):
-                    last = h == H - 1 and ee == 1
+                    first = h == 1 and ee == 0
+                    last = ee == 1
                     if i >= TPG:
                         kv = qkt[:, H + h, (i - TPG) * P : (i + 1) * P].bitcast(BF16)
                         kv = kv.rearrange("p (s r e) -> p s r e", s=SLOTS, e=2)[:, 0 : SLOTS : SLOTS - 1, :, ee]
-                        nc.tensor.matmul(st[:, h, :, :], lhsT=q_half(i, h, ee), rhs=kv, start=False, stop=last)
+                        nc.tensor.matmul(st[:, h, :, :], lhsT=q_half(i, h, ee), rhs=kv, start=first, stop=last)
                     else:
                         nc.tensor.matmul(
-                            st[:, h, 1, :], lhsT=q_half(i, h, ee), rhs=q_half(i, H + h, ee), start=False, stop=last
+                            st[:, h, 1, :], lhsT=q_half(i, h, ee), rhs=q_half(i, H + h, ee), start=first, stop=last
                         )
 
         def score_main(i, h):
@@ -188,8 +192,13 @@ def tile_flexattention_t_kernel(tc, qkv, out):
             mxs[i] = small.tile([P, 2 * H], F32, name="mx")
             negms[i] = small.tile([P, H], F32, name="negm")
             s0 = 0 if i >= TPG else 1
+            tms[i] = work.tile([P, 2, P], F32, name="tm")
+            nc.vector.tensor_tensor(out=tms[i][:, s0:2, :], in0=tris[i][:, 1, s0:2, :], in1=tab_tri1[:, s0:2, :], op=ALU.add)
             nc.vector.tensor_reduce(
-                out=mxs[i][:, 0:H], in_=tris[i][:, :, s0:2, :].rearrange("p h s c -> p h (s c)"), axis=AX.X, op=ALU.max, negate=True
+                out=mxs[i][:, 0:1], in_=tris[i][:, 0, s0:2, :].rearrange("p s c -> p (s c)"), axis=AX.X, op=ALU.max, negate=True
+            )
+            nc.vector.tensor_reduce(
+                out=mxs[i][:, 1:2], in_=tms[i][:, s0:2, :].rearrange("p s c -> p (s c)"), axis=AX.X, op=ALU.max, negate=True
             )
             if i == 0:
                 nc.vector.tensor_scalar(
@@ -223,7 +232,7 @@ def tile_flexattention_t_kernel(tc, qkv, out):
             ev = eb[:, h, base : base + WIN].rearrange("p (s c) -> p s c", s=SLOTS)
             s0 = 0 if i >= TPG else 1
             nc.scalar.activation(
-                out=ev[:, s0 * (SLOTS - 1) : SLOTS : SLOTS - 1, :], in_=tris[i][:, h, s0:2, :], func=ACTF.Exp,
+                out=ev[:, s0 * (SLOTS - 1) : SLOTS : SLOTS - 1, :], in_=(tris[i][:, 0, s0:2, :] if h == 0 else tms[i][:, s0:2, :]), func=ACTF.Exp,
                 bias=negms[i][:, h : h + 1], scale=1.0 / 16.0, accum_out=rss[i][:, h : h + 1],
             )
             if i > 0:
@@ -352,30 +361,30 @@ def tile_flexattention_t_kernel(tc, qkv, out):
                 out=vcodes[:, g, :].bitcast(FP8X4), scales=vscales[:, g, :], in_=vgs[g][:].rearrange("p c t -> p (c t)")
             )
 
-        for i in range(1):
+        for i in range(2):
             flip_qk(i)
             evac_qk(i)
         for j in range(4):
             v_regroup(0, j)
         for n in range(NT + 3):
-            flip_e(n - 2)
+            score_tri(n)
             max_main(n - 1, 1)
             quant(n - 3)
             comb(n - 1, 1)
             expo(n - 1, 0)
+            flip_e(n - 2)
             evac_x(n - 2)
-            evac_y(n - 2)
-            score_tri(n)
-            flip_qk(n + 1)
             score_main(n, 0)
-            max_tri(n)
-            recipro(n - 3)
-            max_main(n, 0)
+            flip_qk(n + 2)
+            evac_qk(n + 2)
             expo(n - 1, 1)
+            max_tri(n)
+            max_main(n, 0)
+            recipro(n - 3)
+            evac_y(n - 2)
             comb(n, 0)
-            evac_qk(n + 1)
-            pv(n - 3)
             score_main(n, 1)
+            pv(n - 3)
             finish(n - 3)
             rsum(n - 1)
             if n == 2 or (n > TPG and n % TPG == 1):

@@ -30,6 +30,7 @@ HE = H * E
 BIG = 2.0 ** 40
 SLOPES = (2.0 ** -4, 2.0 ** -8)
 QK_AHEAD = 8
+WARM_UP = 8
 
 FLOPS = 2 * 2 * E * H * (GROUP * GROUP + (NG - 1) * GROUP * 2 * GROUP)
 
@@ -71,11 +72,10 @@ def tile_flexattention_t_kernel(tc, qkv, out):
                     in_=x[r0 : r0 + 2 * P, 2 * HE : 3 * HE].rearrange("(p e) c -> p e c", e=2),
                 )
 
-        load_qk(0)
-        load_qk(1)
-        load_qk(2)
+        for i in range(5):
+            load_qk(i)
         load_v(0)
-        for i in range(3, QK_AHEAD):
+        for i in range(5, QK_AHEAD):
             load_qk(i)
         load_v(1)
 
@@ -109,6 +109,10 @@ def tile_flexattention_t_kernel(tc, qkv, out):
             nc.vector.tensor_scalar(
                 out=tab_main[:, h, :], in0=dist[:, P : P + MAIN], scalar1=16.0 * SLOPES[h], scalar2=None, op0=ALU.mult
             )
+
+        idle = ps_w.tile([P, 2 * P], F32, name="idle", tag="w")
+        for k in range(WARM_UP):
+            nc.tensor.matmul(idle[:], lhsT=zero[:].bitcast(BF16)[:, 0:P], rhs=zero[:].bitcast(BF16), start=True, stop=True)
 
         qkt = const.tile([P, 2 * H, L], F32, name="qkt")
         vcodes = const.tile([P, NG, HE], U32, name="vcodes", align_bytes=64)
@@ -285,7 +289,7 @@ def tile_flexattention_t_kernel(tc, qkv, out):
         def gr_words(i, s):
             if i not in grs:
                 grs[i] = work.tile([P, 2 * H * P * 4], BF16, name="gr", align_bytes=64)
-            return grs[i][:].bitcast(F32).rearrange("p (s h q u) -> p s h q u", s=2, h=H, q=P)[:, s, :, :, :]
+            return grs[i][:].bitcast(F32).rearrange("p (h s q u) -> p h s q u", s=2, h=H, q=P)[:, :, s, :, :]
 
         def evac_x(i):
             if not ok(i):
@@ -309,10 +313,11 @@ def tile_flexattention_t_kernel(tc, qkv, out):
                 return
             codess[i] = work.tile([P, 2 * H * P], U32, name="codes", align_bytes=64)
             scaless[i] = work.tile([P, 2 * H * P], U8, name="scales", align_bytes=64)
-            c0 = 0 if i >= TPG else H * P
-            nc.vector.quantize_mx(
-                out=codess[i][:, c0:].bitcast(FP8X4), scales=scaless[i][:, c0:], in_=grs[i][:, 4 * c0 :]
-            )
+            spans = [(0, 2 * H * P)] if i >= TPG else [((2 * h + 1) * P, (2 * h + 2) * P) for h in range(H)]
+            for c0, c1 in spans:
+                nc.vector.quantize_mx(
+                    out=codess[i][:, c0:c1].bitcast(FP8X4), scales=scaless[i][:, c0:c1], in_=grs[i][:, 4 * c0 : 4 * c1]
+                )
 
         def pv(i):
             if not ok(i):
@@ -323,7 +328,7 @@ def tile_flexattention_t_kernel(tc, qkv, out):
             passes = [(1, g)] if g == 0 else [(0, g - 1), (1, g)]
             for h in range(H):
                 for n_p, (s, gg) in enumerate(passes):
-                    c0 = (s * H + h) * P
+                    c0 = (h * 2 + s) * P
                     nc.tensor.matmul_mx(
                         out=po[:, h, :], lhsT=codess[i][:, c0 : c0 + P].bitcast(FP8X4), lhsT_scale=scaless[i][:, c0 : c0 + P],
                         rhs=vcodes[:, gg, h * E : (h + 1) * E].bitcast(FP8X4), rhs_scale=vscales[:, gg, h * E : (h + 1) * E],
@@ -361,12 +366,43 @@ def tile_flexattention_t_kernel(tc, qkv, out):
                 out=vcodes[:, g, :].bitcast(FP8X4), scales=vscales[:, g, :], in_=vgs[g][:].rearrange("p c t -> p (c t)")
             )
 
+        last_w = {}
+
+        def last_words(h):
+            return grs[NT - 1][:].bitcast(F32).rearrange("p (h s q u) -> p h s q u", s=2, h=H, q=P)[:, h, :, :, :]
+
+        def last_zero(h, s):
+            last_w[h, s] = ps_s.tile([P, 2, 2, P], F32, name="last_w", tag="s")
+            nc.tensor.transpose(last_w[h, s][:, 0, 0, :], zero[:], ident_f[:])
+
+        def last_flip(h):
+            for j in range(3):
+                w = last_w[h, 0] if h == 0 or j == 0 else last_w[h, 1]
+                s, u = divmod(j + 1, 2)
+                nc.tensor.transpose(w[:, s, u, :], word_block(NT - 1, h, j), ident_f[:])
+
+        def last_quant(h):
+            c0, c1 = 2 * h * P, 2 * (h + 1) * P
+            nc.vector.quantize_mx(
+                out=codess[NT - 1][:, c0:c1].bitcast(FP8X4), scales=scaless[NT - 1][:, c0:c1], in_=grs[NT - 1][:, 4 * c0 : 4 * c1]
+            )
+
+        def last_pv(h):
+            for s in range(2):
+                c0 = (h * 2 + s) * P
+                gg = NG - 2 + s
+                nc.tensor.matmul_mx(
+                    out=last_o[h][:], lhsT=codess[NT - 1][:, c0 : c0 + P].bitcast(FP8X4), lhsT_scale=scaless[NT - 1][:, c0 : c0 + P],
+                    rhs=vcodes[:, gg, h * E : (h + 1) * E].bitcast(FP8X4), rhs_scale=vscales[:, gg, h * E : (h + 1) * E],
+                    start=(s == 0), stop=(s == 1),
+                )
+
         for i in range(2):
             flip_qk(i)
             evac_qk(i)
         for j in range(4):
             v_regroup(0, j)
-        for n in range(NT + 3):
+        for n in range(NT):
             score_tri(n)
             max_main(n - 1, 1)
             quant(n - 3)
@@ -393,3 +429,43 @@ def tile_flexattention_t_kernel(tc, qkv, out):
             load_qk(n + QK_AHEAD)
             if n % TPG == TPG - 1:
                 load_v(n // TPG + 2)
+        grs[NT - 1] = work.tile([P, 2 * H * P * 4], BF16, name="gr", align_bytes=64)
+        codess[NT - 1] = work.tile([P, 2 * H * P], U32, name="codes", align_bytes=64)
+        scaless[NT - 1] = work.tile([P, 2 * H * P], U8, name="scales", align_bytes=64)
+        osb = work.tile([P, H, E], F32, name="osb")
+        last_o = {}
+        max_main(NT - 1, 1)
+        quant(NT - 3)
+        comb(NT - 1, 1)
+        expo(NT - 1, 0)
+        flip_e(NT - 2)
+        last_zero(0, 0)
+        evac_x(NT - 2)
+        evac_y(NT - 2)
+        pv(NT - 3)
+        last_flip(0)
+        expo(NT - 1, 1)
+        recipro(NT - 3)
+        quant(NT - 2)
+        last_w[1, 1] = ps_s.tile([P, 2, 2, P], F32, name="last_w", tag="s")
+        last_zero(1, 0)
+        last_flip(1)
+        nc.vector.tensor_copy(out=last_words(0), in_=last_w[0, 0][:].rearrange("p s u q -> p s q u"))
+        finish(NT - 3)
+        rsum(NT - 1)
+        nc.scalar.copy(out=last_words(1)[:, 1, :, :], in_=last_w[1, 1][:, 1, :, :].rearrange("p u q -> p q u"))
+        nc.vector.tensor_copy(out=last_words(1)[:, 0, :, :], in_=last_w[1, 0][:, 0, :, :].rearrange("p u q -> p q u"))
+        last_quant(0)
+        last_quant(1)
+        recipro(NT - 2)
+        recipro(NT - 1)
+        pv(NT - 2)
+        for h in range(H):
+            last_o[h] = ps_s.tile([P, E], F32, name="last_o", tag="s")
+        last_pv(0)
+        finish(NT - 2)
+        last_pv(1)
+        r = recips[NT - 1]
+        for h in range(H):
+            nc.vector.tensor_tensor(out=osb[:, h, :], in0=last_o[h][:], in1=r[:, h : h + 1].to_broadcast([P, E]), op=ALU.mult)
+            nc.sync.dma_start(out=y[(NT - 1) * P : NT * P, h * E : (h + 1) * E], in_=osb[:, h, :])

@@ -245,14 +245,17 @@ def tile_flexattention_t_kernel(tc, qkv, out):
                     bias=negms[i][:, h : h + 1], scale=1.0 / 16.0, accum_out=rss[i][:, H + h : H + h + 1],
                 )
 
-        def rsum(i):
+        def rsum(i, h):
             if not ok(i):
                 return
             if i == 0:
                 rsums[i] = rss[i]
                 return
-            rsums[i] = small.tile([P, H], F32, name="rsum")
-            nc.gpsimd.tensor_tensor(out=rsums[i][:], in0=rss[i][:, 0:H], in1=rss[i][:, H : 2 * H], op=ALU.add)
+            if h == 0:
+                rsums[i] = small.tile([P, H], F32, name="rsum")
+            nc.gpsimd.tensor_tensor(
+                out=rsums[i][:, h : h + 1], in0=rss[i][:, h : h + 1], in1=rss[i][:, H + h : H + h + 1], op=ALU.add
+            )
 
         def recipro(i):
             if not ok(i):
@@ -422,10 +425,11 @@ def tile_flexattention_t_kernel(tc, qkv, out):
             score_main(n, 1)
             pv(n - 3)
             finish(n - 3)
-            rsum(n - 1)
+            rsum(n - 1, 0)
+            v_regroup(n // TPG + 1, n % TPG)
+            rsum(n - 1, 1)
             if n == 2 or (n > TPG and n % TPG == 1):
                 v_quant(n // TPG)
-            v_regroup(n // TPG + 1, n % TPG)
             load_qk(n + QK_AHEAD)
             if n % TPG == TPG - 1:
                 load_v(n // TPG + 2)
@@ -452,7 +456,8 @@ def tile_flexattention_t_kernel(tc, qkv, out):
         last_flip(1)
         nc.vector.tensor_copy(out=last_words(0), in_=last_w[0, 0][:].rearrange("p s u q -> p s q u"))
         finish(NT - 3)
-        rsum(NT - 1)
+        rsum(NT - 1, 0)
+        rsum(NT - 1, 1)
         nc.scalar.copy(out=last_words(1)[:, 1, :, :], in_=last_w[1, 1][:, 1, :, :].rearrange("p u q -> p q u"))
         nc.vector.tensor_copy(out=last_words(1)[:, 0, :, :], in_=last_w[1, 0][:, 0, :, :].rearrange("p u q -> p q u"))
         last_quant(0)

@@ -25,7 +25,6 @@ NT = L // P
 TPG = GROUP // P
 SLOTS = TPG + 1
 WIN = SLOTS * P
-MAIN = 3 * P
 HE = H * E
 BIG = 2.0 ** 40
 SLOPES = (2.0 ** -4, 2.0 ** -8)
@@ -78,6 +77,7 @@ def tile_flexattention_t_kernel(tc, qkv, out):
         for i in range(5, QK_AHEAD):
             load_qk(i)
         load_v(1)
+        load_v(2)
 
         ident_f = const.tile([P, P], F32, name="ident_f")
         make_identity(nc, ident_f[:])
@@ -96,18 +96,20 @@ def tile_flexattention_t_kernel(tc, qkv, out):
             out=pen[:, 0, :], in0=dist[:, 0:P], scalar1=-256.0, scalar2=-BIG, op0=ALU.is_le, op1=ALU.mult
         )
         nc.vector.tensor_scalar(
-            out=pen[:, 1, :], in0=dist[:, WIN - P : WIN], scalar1=256.0, scalar2=-BIG, op0=ALU.is_gt, op1=ALU.mult
+            out=pen[:, 1, :], in0=dist[:, GROUP:WIN], scalar1=256.0, scalar2=-BIG, op0=ALU.is_gt, op1=ALU.mult
         )
-        tab_tri = const.tile([P, 2, P], BF16, name="tab_tri")
-        tab_tri1 = const.tile([P, 2, P], F32, name="tab_tri1")
-        tab_main = const.tile([P, H, MAIN], BF16, name="tab_main")
+        tab_win = const.tile([P, H, GROUP], BF16, name="tab_win")
+        tab_diag = const.tile([P, H, P], F32, name="tab_diag")
         for h in range(H):
             nc.vector.scalar_tensor_tensor(
-                out=(tab_tri if h == 0 else tab_tri1)[:], in0=dist[:].rearrange("p (s c) -> p s c", s=SLOTS)[:, 0 : SLOTS : SLOTS - 1, :],
-                scalar=16.0 * SLOPES[h], in1=pen[:], op0=ALU.mult, op1=ALU.add,
+                out=tab_diag[:, h, :], in0=dist[:, GROUP:WIN], scalar=16.0 * SLOPES[h], in1=pen[:, 1, :], op0=ALU.mult, op1=ALU.add
+            )
+        for h in range(H):
+            nc.vector.scalar_tensor_tensor(
+                out=tab_win[:, h, 0:P], in0=dist[:, 0:P], scalar=16.0 * SLOPES[h], in1=pen[:, 0, :], op0=ALU.mult, op1=ALU.add
             )
             nc.vector.tensor_scalar(
-                out=tab_main[:, h, :], in0=dist[:, P : P + MAIN], scalar1=16.0 * SLOPES[h], scalar2=None, op0=ALU.mult
+                out=tab_win[:, h, P:GROUP], in0=dist[:, P:GROUP], scalar1=16.0 * SLOPES[h], scalar2=None, op0=ALU.mult
             )
 
         idle = ps_w.tile([P, 2 * P], F32, name="idle", tag="w")
@@ -128,12 +130,11 @@ def tile_flexattention_t_kernel(tc, qkv, out):
             nc.tensor.transpose(yt[:, 2 * b + 1, :], zero[:], ident_f[:])
 
         def live(i):
-            g, a = divmod(i, TPG)
-            return g, a, (max(1, TPG - i))
+            return max(0, TPG - i)
 
-        tps, tris, mains = {}, {}, {}
+        tps, diags, tds, wins = {}, {}, {}, {}
         mxs, negms, rss, rsums, recips = {}, {}, {}, {}, {}
-        tms = {}
+        mws = {}
         xts, grs, codess, scaless, pos = {}, {}, {}, {}, {}
 
         def ok(i):
@@ -155,93 +156,76 @@ def tile_flexattention_t_kernel(tc, qkv, out):
         def q_half(i, h, ee):
             return qkt[:, h, i * P : (i + 1) * P].bitcast(BF16).rearrange("p (r e) -> p r e", e=2)[:, :, ee]
 
-        def score_tri(i):
+        def score_diag(i):
             if not ok(i):
                 return
-            st = ps_s.tile([P, H, 2, P], F32, name="st", tag="s")
-            tris[i] = st
-            for h in (1, 0):
-                if h == 0:
-                    nc.tensor.matmul(
-                        st[:, h, :, :].rearrange("p s c -> p (s c)"), lhsT=ident_b[:],
-                        rhs=tab_tri[:].rearrange("p s c -> p (s c)"), start=True, stop=False,
-                    )
+            sd = ps_s.tile([P, H, P], F32, name="sd", tag="s")
+            diags[i] = sd
+            for h in range(H):
                 for ee in range(2):
-                    first = h == 1 and ee == 0
-                    last = ee == 1
-                    if i >= TPG:
-                        kv = qkt[:, H + h, (i - TPG) * P : (i + 1) * P].bitcast(BF16)
-                        kv = kv.rearrange("p (s r e) -> p s r e", s=SLOTS, e=2)[:, 0 : SLOTS : SLOTS - 1, :, ee]
-                        nc.tensor.matmul(st[:, h, :, :], lhsT=q_half(i, h, ee), rhs=kv, start=first, stop=last)
-                    else:
-                        nc.tensor.matmul(
-                            st[:, h, 1, :], lhsT=q_half(i, h, ee), rhs=q_half(i, H + h, ee), start=first, stop=last
-                        )
+                    nc.tensor.matmul(sd[:, h, :], lhsT=q_half(i, h, ee), rhs=q_half(i, H + h, ee), start=(ee == 0), stop=(ee == 1))
 
-        def score_main(i, h):
+        def score_win(i, h):
             if not ok(i) or i == 0:
                 return
-            g, a, lo = live(i)
-            mt = ps_s.tile([P, MAIN], F32, name="mt", tag="s")
-            mains[i, h] = mt
-            c0 = (lo - 1) * P
-            nc.tensor.matmul(mt[:, c0:MAIN], lhsT=ident_b[:], rhs=tab_main[:, h, c0:MAIN], start=True, stop=False)
+            lo = live(i)
+            sw = ps_s.tile([P, GROUP], F32, name="sw", tag="s")
+            wins[i, h] = sw
+            c0 = lo * P
+            nc.tensor.matmul(sw[:, c0:GROUP], lhsT=ident_b[:], rhs=tab_win[:, h, c0:GROUP], start=True, stop=False)
             kv = qkt[:, H + h, (i - TPG + lo) * P : i * P].bitcast(BF16).rearrange("p (r e) -> p r e", e=2)
             for ee in range(2):
-                nc.tensor.matmul(mt[:, c0:MAIN], lhsT=q_half(i, h, ee), rhs=kv[:, :, ee], start=False, stop=(ee == 1))
+                nc.tensor.matmul(sw[:, c0:GROUP], lhsT=q_half(i, h, ee), rhs=kv[:, :, ee], start=False, stop=(ee == 1))
 
-        def max_tri(i):
+        def bias_diag(i):
+            if not ok(i):
+                return
+            tds[i] = work.tile([P, H, P], F32, name="td")
+            nc.vector.tensor_tensor(out=tds[i][:], in0=diags[i][:], in1=tab_diag[:], op=ALU.add)
+
+        def max_diag(i):
             if not ok(i):
                 return
             mxs[i] = small.tile([P, 2 * H], F32, name="mx")
             negms[i] = small.tile([P, H], F32, name="negm")
-            s0 = 0 if i >= TPG else 1
-            tms[i] = work.tile([P, 2, P], F32, name="tm")
-            nc.vector.tensor_tensor(out=tms[i][:, s0:2, :], in0=tris[i][:, 1, s0:2, :], in1=tab_tri1[:, s0:2, :], op=ALU.add)
-            nc.vector.tensor_reduce(
-                out=mxs[i][:, 0:1], in_=tris[i][:, 0, s0:2, :].rearrange("p s c -> p (s c)"), axis=AX.X, op=ALU.max, negate=True
-            )
-            nc.vector.tensor_reduce(
-                out=mxs[i][:, 1:2], in_=tms[i][:, s0:2, :].rearrange("p s c -> p (s c)"), axis=AX.X, op=ALU.max, negate=True
-            )
+            nc.vector.tensor_reduce(out=mxs[i][:, 0:H], in_=tds[i][:], axis=AX.X, op=ALU.max, negate=True)
             if i == 0:
                 nc.vector.tensor_scalar(
                     out=negms[i][:], in0=mxs[i][:, 0:H], scalar1=1.0 / 16.0, scalar2=None, op0=ALU.mult
                 )
 
-        def max_main(i, h):
+        def max_win(i, h):
             if not ok(i) or i == 0:
                 return
-            g, a, lo = live(i)
+            if h == 0:
+                mws[i] = small.tile([P, H], F32, name="mw")
             nc.vector.tensor_reduce(
-                out=mxs[i][:, H + h : H + h + 1], in_=mains[i, h][:, (lo - 1) * P : MAIN], axis=AX.X, op=ALU.max, negate=True
+                out=mws[i][:, h : h + 1], in_=wins[i, h][:, live(i) * P : GROUP], axis=AX.X, op=ALU.max, negate=True
             )
 
         def comb(i, h):
             if not ok(i) or i == 0:
                 return
             nc.vector.tensor_scalar(
-                out=negms[i][:, h : h + 1], in0=mxs[i][:, h : h + 1], scalar1=mxs[i][:, H + h : H + h + 1],
+                out=negms[i][:, h : h + 1], in0=mxs[i][:, h : h + 1], scalar1=mws[i][:, h : h + 1],
                 scalar2=1.0 / 16.0, op0=ALU.min, op1=ALU.mult,
             )
 
         def expo(i, h):
             if not ok(i):
                 return
-            g, a, lo = live(i)
             if h == 0:
                 rss[i] = small.tile([P, 2 * H], F32, name="rs")
             eb = ebuf[i % 4]
             base = 0 if i % 2 == 0 else P
-            ev = eb[:, h, base : base + WIN].rearrange("p (s c) -> p s c", s=SLOTS)
-            s0 = 0 if i >= TPG else 1
             nc.scalar.activation(
-                out=ev[:, s0 * (SLOTS - 1) : SLOTS : SLOTS - 1, :], in_=(tris[i][:, 0, s0:2, :] if h == 0 else tms[i][:, s0:2, :]), func=ACTF.Exp,
+                out=eb[:, h, base + GROUP : base + WIN], in_=tds[i][:, h, :], func=ACTF.Exp,
                 bias=negms[i][:, h : h + 1], scale=1.0 / 16.0, accum_out=rss[i][:, h : h + 1],
             )
             if i > 0:
+                c0 = live(i) * P
                 nc.scalar.activation(
-                    out=eb[:, h, base + lo * P : base + TPG * P], in_=mains[i, h][:, (lo - 1) * P : MAIN], func=ACTF.Exp,
+                    out=eb[:, h, base + c0 : base + GROUP], in_=wins[i, h][:, c0:GROUP], func=ACTF.Exp,
                     bias=negms[i][:, h : h + 1], scale=1.0 / 16.0, accum_out=rss[i][:, H + h : H + h + 1],
                 )
 
@@ -406,39 +390,40 @@ def tile_flexattention_t_kernel(tc, qkv, out):
         for j in range(4):
             v_regroup(0, j)
         for n in range(NT):
-            score_tri(n)
-            max_main(n - 1, 1)
-            quant(n - 3)
-            comb(n - 1, 1)
+            score_diag(n)
             expo(n - 1, 0)
+            max_win(n - 1, 1)
+            bias_diag(n)
+            comb(n - 1, 1)
+            score_win(n, 0)
+            quant(n - 3)
             flip_e(n - 2)
-            evac_x(n - 2)
-            score_main(n, 0)
-            flip_qk(n + 2)
-            evac_qk(n + 2)
-            expo(n - 1, 1)
-            max_tri(n)
-            max_main(n, 0)
             recipro(n - 3)
-            evac_y(n - 2)
-            comb(n, 0)
-            score_main(n, 1)
+            flip_qk(n + 2)
+            max_win(n, 0)
+            evac_x(n - 2)
+            score_win(n, 1)
+            expo(n - 1, 1)
+            evac_qk(n + 2)
+            max_diag(n)
             pv(n - 3)
             finish(n - 3)
+            evac_y(n - 2)
+            comb(n, 0)
             rsum(n - 1, 0)
             v_regroup(n // TPG + 1, n % TPG)
             rsum(n - 1, 1)
             if n == 2 or (n > TPG and n % TPG == 1):
                 v_quant(n // TPG)
             load_qk(n + QK_AHEAD)
-            if n % TPG == TPG - 1:
-                load_v(n // TPG + 2)
+            if n % TPG == 0:
+                load_v(n // TPG + 3)
         grs[NT - 1] = work.tile([P, 2 * H * P * 4], BF16, name="gr", align_bytes=64)
         codess[NT - 1] = work.tile([P, 2 * H * P], U32, name="codes", align_bytes=64)
         scaless[NT - 1] = work.tile([P, 2 * H * P], U8, name="scales", align_bytes=64)
         osb = work.tile([P, H, E], F32, name="osb")
         last_o = {}
-        max_main(NT - 1, 1)
+        max_win(NT - 1, 1)
         quant(NT - 3)
         comb(NT - 1, 1)
         expo(NT - 1, 0)

@@ -117,6 +117,7 @@ def tile_flexattention_t_kernel(tc, qkv, out):
             nc.tensor.matmul(idle[:], lhsT=zero[:].bitcast(BF16)[:, 0:P], rhs=zero[:].bitcast(BF16), start=True, stop=True)
 
         qkt = const.tile([P, 2 * H, L], F32, name="qkt")
+        kt = const.tile([P, H, 2, L], BF16, name="kt")
         vcodes = const.tile([P, NG, HE], U32, name="vcodes", align_bytes=64)
         vscales = const.tile([P, NG, HE], U8, name="vscales", align_bytes=64)
         ebuf = []
@@ -153,6 +154,20 @@ def tile_flexattention_t_kernel(tc, qkv, out):
                 return
             nc.scalar.copy(out=qkt[:, :, i * P : (i + 1) * P], in_=tps[i][:])
 
+        def part_k(i):
+            if not ok(i):
+                return
+            nc.gpsimd.tensor_scalar(
+                out=kt[:, :, :, i * P : (i + 1) * P],
+                in0=qkt[:, H : 2 * H, i * P : (i + 1) * P].bitcast(BF16).rearrange("p h (r e) -> p h e r", e=2),
+                scalar1=1.0, scalar2=0.0, op0=ALU.mult, op1=ALU.add,
+            )
+
+        def keys(i, h, ee, t0, t1):
+            if i < 10:
+                return qkt[:, H + h, t0 * P : t1 * P].bitcast(BF16).rearrange("p (r e) -> p r e", e=2)[:, :, ee]
+            return kt[:, h, ee, t0 * P : t1 * P]
+
         def q_half(i, h, ee):
             return qkt[:, h, i * P : (i + 1) * P].bitcast(BF16).rearrange("p (r e) -> p r e", e=2)[:, :, ee]
 
@@ -163,7 +178,7 @@ def tile_flexattention_t_kernel(tc, qkv, out):
             diags[i] = sd
             for h in range(H):
                 for ee in range(2):
-                    nc.tensor.matmul(sd[:, h, :], lhsT=q_half(i, h, ee), rhs=q_half(i, H + h, ee), start=(ee == 0), stop=(ee == 1))
+                    nc.tensor.matmul(sd[:, h, :], lhsT=q_half(i, h, ee), rhs=keys(i, h, ee, i, i + 1), start=(ee == 0), stop=(ee == 1))
 
         def score_win(i, h):
             if not ok(i) or i == 0:
@@ -173,9 +188,8 @@ def tile_flexattention_t_kernel(tc, qkv, out):
             wins[i, h] = sw
             c0 = lo * P
             nc.tensor.matmul(sw[:, c0:GROUP], lhsT=ident_b[:], rhs=tab_win[:, h, c0:GROUP], start=True, stop=False)
-            kv = qkt[:, H + h, (i - TPG + lo) * P : i * P].bitcast(BF16).rearrange("p (r e) -> p r e", e=2)
             for ee in range(2):
-                nc.tensor.matmul(sw[:, c0:GROUP], lhsT=q_half(i, h, ee), rhs=kv[:, :, ee], start=False, stop=(ee == 1))
+                nc.tensor.matmul(sw[:, c0:GROUP], lhsT=q_half(i, h, ee), rhs=keys(i, h, ee, i - TPG + lo, i), start=False, stop=(ee == 1))
 
         def bias_diag(i):
             if not ok(i):
@@ -384,7 +398,7 @@ def tile_flexattention_t_kernel(tc, qkv, out):
                     start=(s == 0), stop=(s == 1),
                 )
 
-        for i in range(2):
+        for i in range(3):
             flip_qk(i)
             evac_qk(i)
         for j in range(4):
@@ -399,12 +413,14 @@ def tile_flexattention_t_kernel(tc, qkv, out):
             quant(n - 3)
             flip_e(n - 2)
             recipro(n - 3)
-            flip_qk(n + 2)
+            if n % TPG == 3:
+                v_quant(n // TPG)
+            flip_qk(n + 3)
             max_win(n, 0)
             evac_x(n - 2)
             score_win(n, 1)
             expo(n - 1, 1)
-            evac_qk(n + 2)
+            evac_qk(n + 3)
             max_diag(n)
             pv(n - 3)
             finish(n - 3)
@@ -412,9 +428,9 @@ def tile_flexattention_t_kernel(tc, qkv, out):
             comb(n, 0)
             rsum(n - 1, 0)
             v_regroup(n // TPG + 1, n % TPG)
+            if n >= TPG:
+                part_k(n + 2)
             rsum(n - 1, 1)
-            if n == 2 or (n > TPG and n % TPG == 1):
-                v_quant(n // TPG)
             load_qk(n + QK_AHEAD)
             if n % TPG == 0:
                 load_v(n // TPG + 3)

from contextlib import ExitStack

import concourse.bass as bass
import concourse.mybir as mybir
import concourse.tile as tile
from concourse.masks import make_identity

F32 = mybir.dt.float32
BF16 = mybir.dt.bfloat16
U32 = mybir.dt.uint32
U8 = mybir.dt.uint8
I32 = mybir.dt.int32
FP8X4 = mybir.dt.float8_e4m3fn_x4
ALU = mybir.AluOpType
ACTF = mybir.ActivationFunctionType
AX = mybir.AxisListType

P = 128
L = 4096
H = 2
E = 256
GROUP = 512
NG = L // GROUP
NT = L // P
TPG = GROUP // P
SLOTS = TPG + 1
WIN = SLOTS * P
HE = H * E
BIG = 2.0 ** 40
SLOPES = (2.0 ** -4, 2.0 ** -8)
QK_AHEAD = 8
WARM_UP = 8

FLOPS = 2 * 2 * E * H * (GROUP * GROUP + (NG - 1) * GROUP * 2 * GROUP)


def tile_flexattention_t_kernel(tc, qkv, out):
    nc = tc.nc
    x = qkv.rearrange("b l w h e -> (b l) (w h e)")
    y = out.rearrange("b l h e -> (b l) (h e)")
    with ExitStack() as ctx:
        const = ctx.enter_context(tc.tile_pool(name="const", bufs=1))
        rawp = ctx.enter_context(tc.tile_pool(name="rawp", bufs=QK_AHEAD))
        rawvp = ctx.enter_context(tc.tile_pool(name="rawvp", bufs=3))
        vgp = ctx.enter_context(tc.tile_pool(name="vgp", bufs=2))
        work = ctx.enter_context(tc.tile_pool(name="work", bufs=3))
        ctx.enter_context(tc.manual_schedule())
        small = ctx.enter_context(tc.tile_pool(name="small", bufs=8))
        ps_s = ctx.enter_context(tc.psum_pool(name="ps_s", bufs=5))
        ps_w = ctx.enter_context(tc.psum_pool(name="ps_w", bufs=2))
        ps_y = ctx.enter_context(tc.psum_pool(name="ps_y", bufs=1))

        raws, rawvs, vgs = {}, {}, {}

        def load_qk(i):
            if i >= NT:
                return
            raw = rawp.tile([P, 2 * HE], BF16, name="raw")
            raws[i] = raw
            nc.sync.dma_start(out=raw[:], in_=x[i * P : (i + 1) * P, 0 : 2 * HE])

        def load_v(g):
            if g >= NG:
                return
            rv = rawvp.tile([P, 4, HE], BF16, name="rv")
            rawvs[g] = rv
            for u in range(2):
                r0 = g * GROUP + u * 2 * P
                nc.sync.dma_start(
                    out=rv[:, 2 * u : 2 * u + 2, :],
                    in_=x[r0 : r0 + 2 * P, 2 * HE : 3 * HE].rearrange("(p e) c -> p e c", e=2),
                )

        for i in range(5):
            load_qk(i)
        load_v(0)
        for i in range(5, QK_AHEAD):
            load_qk(i)
        load_v(1)
        load_v(2)

        ident_f = const.tile([P, P], F32, name="ident_f")
        make_identity(nc, ident_f[:])
        dist_i = const.tile([P, WIN], I32, name="dist_i")
        nc.gpsimd.iota(dist_i[:], pattern=[[1, WIN]], base=-2 * P, channel_multiplier=-1)
        ident_b = const.tile([P, P], BF16, name="ident_b")
        make_identity(nc, ident_b[:])
        zero = const.tile([P, P], F32, name="zero")
        nc.vector.memset(zero[:], 0.0)
        warm = const.tile([P, 1], F32, name="warm")
        nc.scalar.activation(out=warm[:], in_=zero[:, 0:1], func=ACTF.Exp)
        dist = const.tile([P, WIN], F32, name="dist")
        nc.vector.tensor_copy(out=dist[:], in_=dist_i[:])
        pen = const.tile([P, 2, P], F32, name="pen")
        nc.vector.tensor_scalar(
            out=pen[:, 0, :], in0=dist[:, 0:P], scalar1=-256.0, scalar2=-BIG, op0=ALU.is_le, op1=ALU.mult
        )
        nc.vector.tensor_scalar(
            out=pen[:, 1, :], in0=dist[:, GROUP:WIN], scalar1=256.0, scalar2=-BIG, op0=ALU.is_gt, op1=ALU.mult
        )
        tab_win = const.tile([P, H, GROUP], BF16, name="tab_win")
        tab_diag = const.tile([P, H, P], F32, name="tab_diag")
        for h in range(H):
            nc.vector.scalar_tensor_tensor(
                out=tab_diag[:, h, :], in0=dist[:, GROUP:WIN], scalar=16.0 * SLOPES[h], in1=pen[:, 1, :], op0=ALU.mult, op1=ALU.add
            )
        for h in range(H):
            nc.vector.scalar_tensor_tensor(
                out=tab_win[:, h, 0:P], in0=dist[:, 0:P], scalar=16.0 * SLOPES[h], in1=pen[:, 0, :], op0=ALU.mult, op1=ALU.add
            )
            nc.vector.tensor_scalar(
                out=tab_win[:, h, P:GROUP], in0=dist[:, P:GROUP], scalar1=16.0 * SLOPES[h], scalar2=None, op0=ALU.mult
            )

        idle = ps_w.tile([P, 2 * P], F32, name="idle", tag="w")
        for k in range(WARM_UP):
            nc.tensor.matmul(idle[:], lhsT=zero[:].bitcast(BF16)[:, 0:P], rhs=zero[:].bitcast(BF16), start=True, stop=True)

        qkt = const.tile([P, 2 * H, L], F32, name="qkt")
        kt = const.tile([P, H, 2, L], BF16, name="kt")
        vcodes = const.tile([P, NG, HE], U32, name="vcodes", align_bytes=64)
        vscales = const.tile([P, NG, HE], U8, name="vscales", align_bytes=64)
        ebuf = []
        for k in range(4):
            eb = const.tile([P, H, 6 * P], BF16, name="eb%d" % k)
            ebuf.append(eb)
            pad = 5 * P if k % 2 == 0 else 0
            nc.vector.memset(eb[:, :, pad : pad + P], 0.0)
        yt = ps_y.tile([P, 2 * H, P], F32, name="yt", tag="y")
        for b in range(H):
            nc.tensor.transpose(yt[:, 2 * b + 1, :], zero[:], ident_f[:])

        def live(i):
            return max(0, TPG - i)

        tps, diags, tds, wins = {}, {}, {}, {}
        mxs, negms, rss, rsums, recips = {}, {}, {}, {}, {}
        mws = {}
        xts, grs, codess, scaless, pos = {}, {}, {}, {}, {}

        def ok(i):
            return 0 <= i < NT

        def flip_qk(i):
            if not ok(i):
                return
            tp = ps_w.tile([P, 2 * H, P], F32, name="tp", tag="w")
            tps[i] = tp
            for j in range(2 * H):
                nc.tensor.transpose(tp[:, j, :], raws[i][:, j * E : (j + 1) * E].bitcast(F32), ident_f[:])

        def evac_qk(i):
            if not ok(i):
                return
            nc.scalar.copy(out=qkt[:, :, i * P : (i + 1) * P], in_=tps[i][:])

        def part_k(i):
            if not ok(i):
                return
            nc.gpsimd.tensor_scalar(
                out=kt[:, :, :, i * P : (i + 1) * P],
                in0=qkt[:, H : 2 * H, i * P : (i + 1) * P].bitcast(BF16).rearrange("p h (r e) -> p h e r", e=2),
                scalar1=1.0, scalar2=0.0, op0=ALU.mult, op1=ALU.add,
            )

        def keys(i, h, ee, t0, t1):
            if i < 10:
                return qkt[:, H + h, t0 * P : t1 * P].bitcast(BF16).rearrange("p (r e) -> p r e", e=2)[:, :, ee]
            return kt[:, h, ee, t0 * P : t1 * P]

        def q_half(i, h, ee):
            return qkt[:, h, i * P : (i + 1) * P].bitcast(BF16).rearrange("p (r e) -> p r e", e=2)[:, :, ee]

        def score_diag(i):
            if not ok(i):
                return
            sd = ps_s.tile([P, H, P], F32, name="sd", tag="s")
            diags[i] = sd
            for h in range(H):
                for ee in range(2):
                    nc.tensor.matmul(sd[:, h, :], lhsT=q_half(i, h, ee), rhs=keys(i, h, ee, i, i + 1), start=(ee == 0), stop=(ee == 1))

        def score_win(i, h):
            if not ok(i) or i == 0:
                return
            lo = live(i)
            sw = ps_s.tile([P, GROUP], F32, name="sw", tag="s")
            wins[i, h] = sw
            c0 = lo * P
            nc.tensor.matmul(sw[:, c0:GROUP], lhsT=ident_b[:], rhs=tab_win[:, h, c0:GROUP], start=True, stop=False)
            for ee in range(2):
                nc.tensor.matmul(sw[:, c0:GROUP], lhsT=q_half(i, h, ee), rhs=keys(i, h, ee, i - TPG + lo, i), start=False, stop=(ee == 1))

        def bias_diag(i):
            if not ok(i):
                return
            tds[i] = work.tile([P, H, P], F32, name="td")
            nc.vector.tensor_tensor(out=tds[i][:], in0=diags[i][:], in1=tab_diag[:], op=ALU.add)

        def max_diag(i):
            if not ok(i):
                return
            mxs[i] = small.tile([P, 2 * H], F32, name="mx")
            negms[i] = small.tile([P, H], F32, name="negm")
            nc.vector.tensor_reduce(out=mxs[i][:, 0:H], in_=tds[i][:], axis=AX.X, op=ALU.max, negate=True)
            if i == 0:
                nc.vector.tensor_scalar(
                    out=negms[i][:], in0=mxs[i][:, 0:H], scalar1=1.0 / 16.0, scalar2=None, op0=ALU.mult
                )

        def max_win(i, h):
            if not ok(i) or i == 0:
                return
            if h == 0:
                mws[i] = small.tile([P, H], F32, name="mw")
            nc.vector.tensor_reduce(
                out=mws[i][:, h : h + 1], in_=wins[i, h][:, live(i) * P : GROUP], axis=AX.X, op=ALU.max, negate=True
            )

        def comb(i, h):
            if not ok(i) or i == 0:
                return
            nc.vector.tensor_scalar(
                out=negms[i][:, h : h + 1], in0=mxs[i][:, h : h + 1], scalar1=mws[i][:, h : h + 1],
                scalar2=1.0 / 16.0, op0=ALU.min, op1=ALU.mult,
            )

        def expo(i, h):
            if not ok(i):
                return
            if h == 0:
                rss[i] = small.tile([P, 2 * H], F32, name="rs")
            eb = ebuf[i % 4]
            base = 0 if i % 2 == 0 else P
            nc.scalar.activation(
                out=eb[:, h, base + GROUP : base + WIN], in_=tds[i][:, h, :], func=ACTF.Exp,
                bias=negms[i][:, h : h + 1], scale=1.0 / 16.0, accum_out=rss[i][:, h : h + 1],
            )
            if i > 0:
                c0 = live(i) * P
                nc.scalar.activation(
                    out=eb[:, h, base + c0 : base + GROUP], in_=wins[i, h][:, c0:GROUP], func=ACTF.Exp,
                    bias=negms[i][:, h : h + 1], scale=1.0 / 16.0, accum_out=rss[i][:, H + h : H + h + 1],
                )

        def rsum(i, h):
            if not ok(i):
                return
            if i == 0:
                rsums[i] = rss[i]
                return
            if h == 0:
                rsums[i] = small.tile([P, H], F32, name="rsum")
            nc.gpsimd.tensor_tensor(
                out=rsums[i][:, h : h + 1], in0=rss[i][:, h : h + 1], in1=rss[i][:, H + h : H + h + 1], op=ALU.add
            )

        def recipro(i):
            if not ok(i):
                return
            recips[i] = small.tile([P, H], F32, name="recip")
            nc.vector.reciprocal(out=recips[i][:], in_=rsums[i][:, 0:H])

        def kind(i):
            g, a = divmod(i, TPG)
            early = a < 2
            xw, yw = ((0, 1), 2) if early else ((1, 2), 0)
            xs, ys = (0, 1) if early else (1, 0)
            has_x = g > 0 or not early
            has_y = g > 0 or early
            return early, xw, yw, xs, ys, has_x, has_y

        def word_block(i, h, j):
            return ebuf[i % 4][:, h, 2 * P * j : 2 * P * (j + 1)].bitcast(F32)

        def flip_e(i):
            if not ok(i):
                return
            early, xw, yw, xs, ys, has_x, has_y = kind(i)
            if has_x:
                xt = ps_w.tile([P, 2 * H, P], F32, name="xt", tag="w")
                xts[i] = xt
                for h in range(H):
                    for u in range(2):
                        nc.tensor.transpose(xt[:, 2 * h + u, :], word_block(i, h, xw[u]), ident_f[:])
            if has_y:
                for h in range(H):
                    nc.tensor.transpose(yt[:, 2 * h, :], word_block(i, h, yw), ident_f[:])

        def gr_words(i, s):
            if i not in grs:
                grs[i] = work.tile([P, 2 * H * P * 4], BF16, name="gr", align_bytes=64)
            return grs[i][:].bitcast(F32).rearrange("p (h s q u) -> p h s q u", s=2, h=H, q=P)[:, :, s, :, :]

        def evac_x(i):
            if not ok(i):
                return
            early, xw, yw, xs, ys, has_x, has_y = kind(i)
            if has_x:
                nc.scalar.copy(out=gr_words(i, xs), in_=xts[i][:].rearrange("p (h u) q -> p h q u", h=H))

        def evac_y(i):
            if not ok(i):
                return
            early, xw, yw, xs, ys, has_x, has_y = kind(i)
            if has_y:
                yv = yt[:].rearrange("p (h u) q -> p h u q", h=H)
                if not early:
                    yv = yv[:, :, ::-1, :]
                nc.vector.tensor_copy(out=gr_words(i, ys), in_=yv.rearrange("p h u q -> p h q u"))

        def quant(i):
            if not ok(i):
                return
            codess[i] = work.tile([P, 2 * H * P], U32, name="codes", align_bytes=64)
            scaless[i] = work.tile([P, 2 * H * P], U8, name="scales", align_bytes=64)
            spans = [(0, 2 * H * P)] if i >= TPG else [((2 * h + 1) * P, (2 * h + 2) * P) for h in range(H)]
            for c0, c1 in spans:
                nc.vector.quantize_mx(
                    out=codess[i][:, c0:c1].bitcast(FP8X4), scales=scaless[i][:, c0:c1], in_=grs[i][:, 4 * c0 : 4 * c1]
                )

        def pv(i):
            if not ok(i):
                return
            g, a = divmod(i, TPG)
            po = ps_w.tile([P, H, E], F32, name="po", tag="w")
            pos[i] = po
            passes = [(1, g)] if g == 0 else [(0, g - 1), (1, g)]
            for h in range(H):
                for n_p, (s, gg) in enumerate(passes):
                    c0 = (h * 2 + s) * P
                    nc.tensor.matmul_mx(
                        out=po[:, h, :], lhsT=codess[i][:, c0 : c0 + P].bitcast(FP8X4), lhsT_scale=scaless[i][:, c0 : c0 + P],
                        rhs=vcodes[:, gg, h * E : (h + 1) * E].bitcast(FP8X4), rhs_scale=vscales[:, gg, h * E : (h + 1) * E],
                        start=(n_p == 0), stop=(n_p == len(passes) - 1),
                    )

        def finish(i):
            if not ok(i):
                return
            osb = work.tile([P, H, E], F32, name="osb")
            if i == NT - 1:
                nc.vector.tensor_tensor(
                    out=osb[:], in0=pos[i][:], in1=recips[i][:].unsqueeze(2).to_broadcast([P, H, E]), op=ALU.mult
                )
            else:
                for h in range(H):
                    nc.scalar.activation(out=osb[:, h, :], in_=pos[i][:, h, :], func=ACTF.Copy, scale=recips[i][:, h : h + 1])
            nc.sync.dma_start(out=y[i * P : (i + 1) * P, :], in_=osb[:].rearrange("p h e -> p (h e)"))

        def v_regroup(g, j):
            if g >= NG:
                return
            if j == 0:
                vgs[g] = vgp.tile([P, HE, 4], BF16, name="vg", align_bytes=64)
            c0 = j * P
            nc.gpsimd.tensor_scalar(
                out=vgs[g][:, c0 : c0 + P, :], in0=rawvs[g][:, :, c0 : c0 + P].rearrange("p t c -> p c t"),
                scalar1=1.0, scalar2=0.0, op0=ALU.mult, op1=ALU.add,
            )

        def v_quant(g):
            if g >= NG:
                return
            nc.vector.quantize_mx(
                out=vcodes[:, g, :].bitcast(FP8X4), scales=vscales[:, g, :], in_=vgs[g][:].rearrange("p c t -> p (c t)")
            )

        last_w = {}

        def last_words(h):
            return grs[NT - 1][:].bitcast(F32).rearrange("p (h s q u) -> p h s q u", s=2, h=H, q=P)[:, h, :, :, :]

        def last_zero(h, s):
            last_w[h, s] = ps_s.tile([P, 2, 2, P], F32, name="last_w", tag="s")
            nc.tensor.transpose(last_w[h, s][:, 0, 0, :], zero[:], ident_f[:])

        def last_flip(h):
            for j in range(3):
                w = last_w[h, 0] if h == 0 or j == 0 else last_w[h, 1]
                s, u = divmod(j + 1, 2)
                nc.tensor.transpose(w[:, s, u, :], word_block(NT - 1, h, j), ident_f[:])

        def last_quant(h):
            c0, c1 = 2 * h * P, 2 * (h + 1) * P
            nc.vector.quantize_mx(
                out=codess[NT - 1][:, c0:c1].bitcast(FP8X4), scales=scaless[NT - 1][:, c0:c1], in_=grs[NT - 1][:, 4 * c0 : 4 * c1]
            )

        def last_pv(h):
            for s in range(2):
                c0 = (h * 2 + s) * P
                gg = NG - 2 + s
                nc.tensor.matmul_mx(
                    out=last_o[h][:], lhsT=codess[NT - 1][:, c0 : c0 + P].bitcast(FP8X4), lhsT_scale=scaless[NT - 1][:, c0 : c0 + P],
                    rhs=vcodes[:, gg, h * E : (h + 1) * E].bitcast(FP8X4), rhs_scale=vscales[:, gg, h * E : (h + 1) * E],
                    start=(s == 0), stop=(s == 1),
                )

        for i in range(3):
            flip_qk(i)
            evac_qk(i)
        for j in range(4):
            v_regroup(0, j)
        for n in range(NT):
            score_diag(n)
            expo(n - 1, 0)
            max_win(n - 1, 1)
            bias_diag(n)
            comb(n - 1, 1)
            score_win(n, 0)
            quant(n - 3)
            flip_e(n - 2)
            recipro(n - 3)
            if n % TPG == 3:
                v_quant(n // TPG)
            flip_qk(n + 3)
            max_win(n, 0)
            evac_x(n - 2)
            score_win(n, 1)
            expo(n - 1, 1)
            evac_qk(n + 3)
            max_diag(n)
            pv(n - 3)
            finish(n - 3)
            evac_y(n - 2)
            comb(n, 0)
            rsum(n - 1, 0)
            v_regroup(n // TPG + 1, n % TPG)
            if n >= TPG:
                part_k(n + 2)
            rsum(n - 1, 1)
            load_qk(n + QK_AHEAD)
            if n % TPG == 0:
                load_v(n // TPG + 3)
        grs[NT - 1] = work.tile([P, 2 * H * P * 4], BF16, name="gr", align_bytes=64)
        codess[NT - 1] = work.tile([P, 2 * H * P], U32, name="codes", align_bytes=64)
        scaless[NT - 1] = work.tile([P, 2 * H * P], U8, name="scales", align_bytes=64)
        osb = work.tile([P, H, E], F32, name="osb")
        last_o = {}
        max_win(NT - 1, 1)
        quant(NT - 3)
        comb(NT - 1, 1)
        expo(NT - 1, 0)
        flip_e(NT - 2)
        last_zero(0, 0)
        evac_x(NT - 2)
        evac_y(NT - 2)
        pv(NT - 3)
        last_flip(0)
        expo(NT - 1, 1)
        recipro(NT - 3)
        quant(NT - 2)
        last_w[1, 1] = ps_s.tile([P, 2, 2, P], F32, name="last_w", tag="s")
        last_zero(1, 0)
        last_flip(1)
        nc.vector.tensor_copy(out=last_words(0), in_=last_w[0, 0][:].rearrange("p s u q -> p s q u"))
        finish(NT - 3)
        rsum(NT - 1, 0)
        rsum(NT - 1, 1)
        nc.scalar.copy(out=last_words(1)[:, 1, :, :], in_=last_w[1, 1][:, 1, :, :].rearrange("p u q -> p q u"))
        nc.vector.tensor_copy(out=last_words(1)[:, 0, :, :], in_=last_w[1, 0][:, 0, :, :].rearrange("p u q -> p q u"))
        last_quant(0)
        last_quant(1)
        recipro(NT - 2)
        recipro(NT - 1)
        pv(NT - 2)
        for h in range(H):
            last_o[h] = ps_s.tile([P, E], F32, name="last_o", tag="s")
        last_pv(0)
        finish(NT - 2)
        last_pv(1)
        r = recips[NT - 1]
        for h in range(H):
            nc.vector.tensor_tensor(out=osb[:, h, :], in0=last_o[h][:], in1=r[:, h : h + 1].to_broadcast([P, E]), op=ALU.mult)
            nc.sync.dma_start(out=y[(NT - 1) * P : NT * P, h * E : (h + 1) * E], in_=osb[:, h, :])
